import numpy as np
import ml_dtypes


def mxq(x, axis, fmt="e4m3"):
    dtype, down = {"e4m3": (ml_dtypes.float8_e4m3fn, 7), "e5m2": (ml_dtypes.float8_e5m2, 14)}[fmt]
    v = np.moveaxis(np.asarray(x, np.float32).astype(ml_dtypes.bfloat16).astype(np.float64), axis, -1)
    blocks = v.reshape(v.shape[:-1] + (-1, 32))
    amax = np.abs(blocks).max(-1, keepdims=True)
    byte = np.maximum(np.where(amax > 0, np.frexp(amax)[1] - 1 + 127, 0) - down, 1)
    scale = np.exp2(byte - 127.0)
    codes = (blocks / scale).astype(np.float32).astype(dtype).astype(np.float64)
    return np.moveaxis((codes * scale).reshape(v.shape), -1, axis)


WIDE = False


def mx_kscale(k):
    if not WIDE:
        return np.ones(k)
    levels = np.array([10, -10, 5, -5, 0])
    if k % 512:
        return np.exp2(np.random.permutation(np.resize(levels, k // 32))).repeat(32)
    a = np.empty((k // 512, 16))
    for p in range(k // 512):
        a[p, :8] = np.random.permutation(np.resize(levels, 8))
        for g in range(8):
            far = levels[np.abs(levels - a[p, g]) >= 10]
            a[p, g + 8] = far[np.random.randint(len(far))]
    return np.exp2(a.ravel()).repeat(32)


BF16 = ml_dtypes.bfloat16


def bf(x):
    return np.asarray(x, np.float32).astype(BF16)


def f64(x):
    return np.asarray(x).astype(np.float64)


N, D, B = 4096, 256, 3072


def setup_inputs():
    f = np.concatenate([np.ones(B), mx_kscale(N)[B:]])
    g = np.mean(f)
    return {"adjacency_matrix": bf(np.random.uniform(size=(N, N)) * f[None, :]),
            "node_features": bf(np.random.standard_normal((N, D)) / f[:, None]),
            "W_gcn": bf(np.random.standard_normal((D, D)) * 0.25 * np.sqrt(N) / np.sqrt(D) * g),
            "W_skip": bf(np.random.standard_normal((D, D)) * 0.5 / np.sqrt(D)),
            "batch_size": B}


def reference(adjacency_matrix, node_features, W_gcn, W_skip, batch_size):
    beta = 0.5
    a = f64(adjacency_matrix)
    x = f64(node_features)
    deg = np.sum(a, axis=1)
    d_inv_sqrt = 1.0 / np.sqrt(deg + 1e-8)
    normalized_adj = d_inv_sqrt[:, None] * a * d_inv_sqrt[None, :]
    h = x @ f64(W_gcn).T
    adj_rows = normalized_adj[:batch_size]
    gcn_out = np.maximum((mxq(adj_rows, 1, "e4m3") @ mxq(h, 0, "e4m3")) + x[:batch_size] @ f64(W_skip).T, 0.0)
    sample_features = gcn_out[:batch_size]
    original_features = x[:batch_size]
    enhanced_features = original_features + beta * sample_features
    return enhanced_features

@@ -1,0 +1,277 @@
+from contextlib import ExitStack
+
+import concourse.bass as bass
+import concourse.mybir as mybir
+import concourse.tile as tile
+from concourse.masks import make_identity
+
+F32 = mybir.dt.float32
+BF16 = mybir.dt.bfloat16
+U8 = mybir.dt.uint8
+U32 = mybir.dt.uint32
+FP8X4 = mybir.dt.float8_e4m3fn_x4
+ALU = mybir.AluOpType
+ACT = mybir.ActivationFunctionType
+
+P = 128
+NODES = 4096
+FEAT = 256
+ROWS = 3072
+NBLK = NODES // P
+MBLK = ROWS // P
+PASS = 512
+NPASS = NODES // PASS
+NCHUNK = ROWS // PASS
+OPEN = [0, 1]
+A_SLOTS = 9
+LAG = 2
+FIN_DELAY = 2
+PREP_AT = 3
+
+FLOPS = 2 * ROWS * NODES * FEAT + 2 * NODES * FEAT * FEAT + 2 * ROWS * FEAT * FEAT
+
+
+def make_tokens():
+    toks = [("loadx",)]
+    for c in range(NPASS):
+        toks.append(("load", c, 0))
+    rest = [m for m in range(NCHUNK) if m not in OPEN]
+    for m in rest:
+        toks.append(("load", m, 1))
+    toks.append(("feat",))
+    known = []
+    for c in range(NPASS):
+        toks.append(("rows", c))
+        known.append(c)
+        for m in OPEN:
+            if m == c:
+                toks.append(("prep", m))
+                toks.extend([("pair", m, g, 1) for g in known])
+            elif m in known:
+                toks.append(("pair", m, c, 1))
+    for i, m in enumerate(rest):
+        if i == 0:
+            toks.append(("prep", m))
+        for g in range(NPASS):
+            toks.append(("pair", m, g, 2))
+            if g == PREP_AT and i + 1 < len(rest):
+                toks.append(("prep", rest[i + 1]))
+    toks.append(("drain",))
+    return toks
+
+
+def tile_structureawaregcn_t_kernel(tc, adjacency_matrix, node_features, W_gcn, W_skip, batch_size, out):
+    nc = tc.nc
+    a_groups = adjacency_matrix.rearrange("(g q s e) n -> g s q e n", q=P, s=2, e=2)
+    x_groups = node_features.rearrange("(g q t) d -> q g t d", q=P, t=4)
+    out_groups = out.rearrange("(g q s e) c -> g s q e c", q=P, s=2, e=2)
+    with ExitStack() as ctx:
+        const = ctx.enter_context(tc.tile_pool(name="const", bufs=1))
+        apool = ctx.enter_context(tc.tile_pool(name="apool", bufs=A_SLOTS))
+        ppool = ctx.enter_context(tc.tile_pool(name="ppool", bufs=4))
+        gpool = ctx.enter_context(tc.tile_pool(name="gpool", bufs=4))
+        cpool = ctx.enter_context(tc.tile_pool(name="cpool", bufs=3))
+        dpool = ctx.enter_context(tc.tile_pool(name="dpool", bufs=3))
+        epool = ctx.enter_context(tc.tile_pool(name="epool", bufs=2))
+        psum = ctx.enter_context(tc.psum_pool(name="psum", bufs=4))
+        ctx.enter_context(tc.manual_schedule())
+
+        ident_f = const.tile([P, P], F32, name="ident_f")
+        ident_b = const.tile([P, P], BF16, name="ident_b")
+        make_identity(nc, ident_b[:])
+        make_identity(nc, ident_f[:])
+        wT = const.tile([P, 2, 2, FEAT], BF16, name="wT")
+        hc = const.tile([P, NPASS, FEAT], U32, name="hc", align_bytes=64)
+        hs = const.tile([P, NPASS, FEAT], U8, name="hs", align_bytes=64)
+        xT = const.tile([P, 2, ROWS], BF16, name="xT")
+        deg = const.tile([P, NBLK, 8], F32, name="deg")
+        sq = const.tile([P, NBLK], F32, name="sq")
+        dinv = const.tile([P, NBLK], F32, name="dinv")
+        warm = const.tile([P, 1], F32, name="warm")
+        nc.vector.memset(warm[:], 1.0)
+        nc.scalar.activation(out=warm[:], in_=warm[:], func=ACT.Sqrt)
+
+        first = {}
+        second = {}
+        st = {"x": None}
+
+        scratch = apool.tile([P, 2, NODES], BF16, name="scratch", tag="a", align_bytes=64)
+        w_nat = scratch[:, 0, 3072:4096].rearrange("p (w h d) -> p w h d", w=2, h=2)
+        xT_tail = scratch[:, 0, 0:2048].rearrange("p (h n) -> p h n", h=2)
+        nc.sync.dma_start(out=w_nat[:, 0], in_=W_gcn.rearrange("(h p) d -> p h d", p=P))
+        nc.sync.dma_start(out=w_nat[:, 1], in_=W_skip.rearrange("(h p) d -> p h d", p=P))
+
+        def load_x():
+            x_t = apool.tile([P, 2, NODES], BF16, name="x_t", tag="a", align_bytes=64)
+            st["x"] = x_t[:].rearrange("p a n -> p (a n)")
+            nc.sync.dma_start(out=st["x"].rearrange("p (g t d) -> p g t d", t=4, d=FEAT), in_=x_groups)
+
+        def load_chunk(c, again):
+            for G in range(2 * c, 2 * c + 2):
+                a_t = apool.tile([P, 2, NODES], BF16, name="a_t", tag="a", align_bytes=64)
+                nc.sync.dma_start(out=a_t[:], in_=a_groups[c, G % 2])
+                for e in range(2):
+                    (second if again else first)[2 * G + e] = a_t[:, e, :]
+
+        def degrees(c):
+            for blk in range(4 * c, 4 * c + 4):
+                a_b = first[blk]
+                if blk % 2 == 0:
+                    nc.vector.tensor_scalar(out=a_b, in0=a_b, scalar1=1.0, scalar2=None, op0=ALU.mult, op1=ALU.add, accum_out=deg[:, blk, 0:1])
+                else:
+                    nc.scalar.activation(out=a_b, in_=a_b, func=ACT.Copy, accum_out=deg[:, blk, 0:1])
+            cols = slice(4 * c, 4 * c + 4)
+            nc.scalar.activation(out=sq[:, cols], in_=deg[:, cols, 0], func=ACT.Sqrt, bias=1e-8)
+            nc.vector.reciprocal(out=dinv[:, cols], in_=sq[:, cols])
+
+        def features():
+            x_flat = st["x"]
+            wps = psum.tile([P, 2, 2, 2, P], BF16, name="wps", tag="T")
+            for w in range(2):
+                for dh in range(2):
+                    for oh in range(2):
+                        nc.tensor.transpose(wps[:, w, dh, oh, :], w_nat[:, w, oh, P * dh : P * dh + P], ident_b[:])
+            nc.scalar.copy(out=wT[:].rearrange("p w h o -> p (w h o)"), in_=wps[:].rearrange("p w h q o -> p (w h q o)"))
+            for q in range(4):
+                for dh in range(2):
+                    xps = psum.tile([P, 8, P], BF16, name="xps", tag="T")
+                    for nb in range(8):
+                        col = FEAT * (8 * q + nb) + P * dh
+                        nc.tensor.transpose(xps[:, nb, :], x_flat[:, col : col + P], ident_b[:])
+                    dst = xT[:, dh, 1024 * q : 1024 * q + 1024] if q < 3 else xT_tail[:, dh, :]
+                    if dh == 0:
+                        nc.scalar.copy(out=dst, in_=xps[:].rearrange("p b n -> p (b n)"))
+                    else:
+                        nc.vector.tensor_copy(out=dst, in_=xps[:].rearrange("p b n -> p (b n)"))
+            for g in range(NPASS):
+                gh = x_flat[:, 1024 * g : 1024 * g + 1024].rearrange("p (c t) -> p c t", t=4)
+                for ch in range(2):
+                    hps = psum.tile([P, 4, P], F32, name="hps", tag="T")
+                    for t in range(4):
+                        blk = 4 * g + t
+                        for dh in range(2):
+                            lhsT = xT[:, dh, P * blk : P * blk + P] if blk < MBLK else xT_tail[:, dh, P * (blk - MBLK) : P * (blk - MBLK) + P]
+                            nc.tensor.matmul(out=hps[:, t, :], lhsT=lhsT, rhs=wT[:, 0, dh, P * ch : P * ch + P], start=(dh == 0), stop=(dh == 1))
+                    nc.vector.tensor_copy(out=gh[:, P * ch : P * ch + P, :], in_=hps[:].rearrange("p t c -> p c t"))
+                nc.vector.quantize_mx(out=hc[:, g, :].bitcast(FP8X4), scales=hs[:, g, :], in_=x_flat[:, 1024 * g : 1024 * g + 1024])
+
+        toks = make_tokens()
+        pairs = [t for t in toks if t[0] == "pair"]
+        work = [{} for t in pairs]
+        acc = {}
+        seen = {}
+        drow = {}
+        wsm = {}
+        fin = []
+
+        def prep(m):
+            dps = psum.tile([P, 4, P], F32, name="dps", tag="T")
+            for j in range(4):
+                b = 4 * m + j
+                nc.tensor.transpose(dps[:, j, :], dinv[:, b : b + 1].to_broadcast([P, P]), ident_f[:])
+            dr = dpool.tile([P, PASS], F32, name="dr")
+            nc.scalar.copy(out=dr[:], in_=dps[:].rearrange("p j r -> p (j r)"))
+            drow[m] = dr
+            ws = []
+            for ch in range(2):
+                skp = psum.tile([P, PASS], F32, name="skp", tag="T")
+                for dh in range(2):
+                    nc.tensor.matmul(out=skp[:], lhsT=wT[:, 1, dh, P * ch : P * ch + P], rhs=xT[:, dh, PASS * m : PASS * m + PASS], start=(dh == 0), stop=(dh == 1))
+                w = epool.tile([P, PASS], F32, name="w%d" % ch)
+                nc.scalar.activation(out=w[:], in_=skp[:], func=ACT.Copy, scale=0.5)
+                ws.append(w)
+            wsm[m] = ws
+
+        def stage_t(k):
+            if k >= len(pairs):
+                return
+            m, g, ph = pairs[k][1], pairs[k][2], pairs[k][3]
+            src = second if ph == 2 else first
+            banks = []
+            for u in range(2):
+                bank = psum.tile([P, 4, P], F32, name="bank", tag="T")
+                for j in range(4):
+                    nc.tensor.transpose(bank[:, j, :], src[4 * m + j].bitcast(F32)[:, 256 * g + u : 256 * g + 256 : 2], ident_f[:])
+                banks.append(bank)
+            work[k]["banks"] = banks
+
+        def stage_v(k):
+            m, g = pairs[k][1], pairs[k][2]
+            planes = ppool.tile([P, 4, PASS], BF16, name="planes")
+            for u in range(2):
+                halves = work[k]["banks"][u][:].rearrange("p j r -> p (j r)").bitcast(BF16).rearrange("p (x e) -> p x e", e=2)
+                for e in range(2):
+                    t = 2 * u + e
+                    nc.vector.scalar_tensor_tensor(out=planes[:, t, :], in0=halves[:, :, e], scalar=dinv[:, 4 * g + t : 4 * g + t + 1], in1=drow[m][:], op0=ALU.mult, op1=ALU.mult)
+            work[k]["planes"] = planes
+
+        def stage_r(k):
+            planes = work[k]["planes"]
+            grp = gpool.tile([P, PASS, 4], BF16, name="grp", align_bytes=64)
+            if pairs[k][3] == 1:
+                nc.gpsimd.tensor_scalar(out=grp[:], in0=planes[:].rearrange("p t x -> p x t"), scalar1=1.0, scalar2=0.0, op0=ALU.mult, op1=ALU.add)
+            else:
+                nc.scalar.copy(out=grp[:].rearrange("p (c i) t -> p c t i", i=4), in_=planes[:].rearrange("p t (c i) -> p c t i", i=4))
+            work[k]["grp"] = grp
+
+        def stage_q(k):
+            m, g = pairs[k][1], pairs[k][2]
+            if m not in acc:
+                acc[m] = [psum.tile([P, PASS], F32, name="acc", tag="acc") for ch in range(2)]
+            codes = cpool.tile([P, PASS], U32, name="codes", align_bytes=64)
+            scl = cpool.tile([P, PASS], U8, name="scl", align_bytes=64)
+            nc.vector.quantize_mx(out=codes[:].bitcast(FP8X4), scales=scl[:], in_=work[k]["grp"][:].rearrange("p x t -> p (x t)"))
+            seen[m] = seen.get(m, 0) + 1
+            for ch in range(2):
+                nc.tensor.matmul_mx(out=acc[m][ch][:], lhsT=hc[:, g, P * ch : P * ch + P].bitcast(FP8X4), lhsT_scale=hs[:, g, P * ch : P * ch + P], rhs=codes[:].bitcast(FP8X4), rhs_scale=scl[:], start=(seen[m] == 1), stop=(seen[m] == NPASS))
+            if seen[m] == NPASS:
+                fin.append((m, k + FIN_DELAY))
+
+        def finish(m):
+            ws = wsm[m]
+            for ch in range(2):
+                w = ws[ch]
+                nc.vector.scalar_tensor_tensor(out=w[:], in0=acc[m][ch][:], scalar=0.5, in1=w[:], op0=ALU.mult, op1=ALU.add)
+                nc.vector.scalar_tensor_tensor(out=w[:], in0=w[:], scalar=0.0, in1=xT[:, ch, PASS * m : PASS * m + PASS], op0=ALU.max, op1=ALU.add)
+            for jp in range(2):
+                bo = psum.tile([P, 2, 2, P], F32, name="bo", tag="T")
+                for e in range(2):
+                    for ch in range(2):
+                        col = P * (2 * jp + e)
+                        nc.tensor.transpose(bo[:, e, ch, :], ws[ch][:, col : col + P], ident_f[:])
+                o = epool.tile([P, 2, FEAT], F32, name="o")
+                nc.scalar.copy(out=o[:].rearrange("p e c -> p (e c)"), in_=bo[:].rearrange("p e h c -> p (e h c)"))
+                nc.scalar.dma_start(out=out_groups[m, jp], in_=o[:])
+
+        k = 0
+        qd = 0
+        for tok in toks:
+            kind = tok[0]
+            if kind == "loadx":
+                load_x()
+            elif kind == "load":
+                load_chunk(tok[1], tok[2])
+            elif kind == "feat":
+                features()
+            elif kind == "rows":
+                degrees(tok[1])
+            elif kind == "prep":
+                prep(tok[1])
+            elif kind == "pair":
+                if k == 0:
+                    stage_t(0)
+                stage_t(k + 1)
+                stage_v(k)
+                stage_r(k)
+                if k - LAG >= qd:
+                    stage_q(qd)
+                    qd += 1
+                k += 1
+                while fin and fin[0][1] <= k:
+                    finish(fin.pop(0)[0])
+            else:
+                while qd < k:
+                    stage_q(qd)
+                    qd += 1
+                while fin:
+                    finish(fin.pop(0)[0])

@@ -1,8 +1,6 @@
 from contextlib import ExitStack
 
-import concourse.bass as bass
 import concourse.mybir as mybir
-import concourse.tile as tile
 from concourse.masks import make_identity
 
 F32 = mybir.dt.float32
@@ -17,261 +15,271 @@ P = 128
 NODES = 4096
 FEAT = 256
 ROWS = 3072
-NBLK = NODES // P
-MBLK = ROWS // P
-PASS = 512
-NPASS = NODES // PASS
-NCHUNK = ROWS // PASS
-OPEN = [0, 1]
-A_SLOTS = 9
-LAG = 2
-FIN_DELAY = 2
-PREP_AT = 3
+T = 4
+CHUNKS = NODES // (P * T)
+OUT_TILES = ROWS // P
+RES_TILES = 16
+PAIR = 1024
+NPAIR = NODES // PAIR
+LAG_T = 1
+LAG_C = 2
 
 FLOPS = 2 * ROWS * NODES * FEAT + 2 * NODES * FEAT * FEAT + 2 * ROWS * FEAT * FEAT
 
 
-def make_tokens():
-    toks = [("loadx",)]
-    for c in range(NPASS):
-        toks.append(("load", c, 0))
-    rest = [m for m in range(NCHUNK) if m not in OPEN]
-    for m in rest:
-        toks.append(("load", m, 1))
-    toks.append(("feat",))
-    known = []
-    for c in range(NPASS):
-        toks.append(("rows", c))
-        known.append(c)
-        for m in OPEN:
-            if m == c:
-                toks.append(("prep", m))
-                toks.extend([("pair", m, g, 1) for g in known])
-            elif m in known:
-                toks.append(("pair", m, c, 1))
-    for i, m in enumerate(rest):
-        if i == 0:
-            toks.append(("prep", m))
-        for g in range(NPASS):
-            toks.append(("pair", m, g, 2))
-            if g == PREP_AT and i + 1 < len(rest):
-                toks.append(("prep", rest[i + 1]))
-    toks.append(("drain",))
-    return toks
-
-
 def tile_structureawaregcn_t_kernel(tc, adjacency_matrix, node_features, W_gcn, W_skip, batch_size, out):
     nc = tc.nc
-    a_groups = adjacency_matrix.rearrange("(g q s e) n -> g s q e n", q=P, s=2, e=2)
-    x_groups = node_features.rearrange("(g q t) d -> q g t d", q=P, t=4)
-    out_groups = out.rearrange("(g q s e) c -> g s q e c", q=P, s=2, e=2)
+    a_rows = adjacency_matrix.rearrange("(g p t) n -> g p t n", p=P, t=T)
+    x_rows = node_features.rearrange("(g p t) d -> p g t d", p=P, t=T)
+    out_rows = out.rearrange("(g p t) c -> g p t c", p=P, t=T)
     with ExitStack() as ctx:
         const = ctx.enter_context(tc.tile_pool(name="const", bufs=1))
-        apool = ctx.enter_context(tc.tile_pool(name="apool", bufs=A_SLOTS))
-        ppool = ctx.enter_context(tc.tile_pool(name="ppool", bufs=4))
-        gpool = ctx.enter_context(tc.tile_pool(name="gpool", bufs=4))
-        cpool = ctx.enter_context(tc.tile_pool(name="cpool", bufs=3))
-        dpool = ctx.enter_context(tc.tile_pool(name="dpool", bufs=3))
-        epool = ctx.enter_context(tc.tile_pool(name="epool", bufs=2))
-        psum = ctx.enter_context(tc.psum_pool(name="psum", bufs=4))
+        rpool = ctx.enter_context(tc.tile_pool(name="rpool", bufs=RES_TILES))
+        spool = ctx.enter_context(tc.tile_pool(name="spool", bufs=4))
+        cpool = ctx.enter_context(tc.tile_pool(name="cpool", bufs=2))
+        epool = ctx.enter_context(tc.tile_pool(name="epool", bufs=3))
+        psum_t = ctx.enter_context(tc.psum_pool(name="psum_t", bufs=4))
+        psum_a = ctx.enter_context(tc.psum_pool(name="psum_a", bufs=2))
+        psum_k = ctx.enter_context(tc.psum_pool(name="psum_k", bufs=2))
         ctx.enter_context(tc.manual_schedule())
 
         ident_f = const.tile([P, P], F32, name="ident_f")
         ident_b = const.tile([P, P], BF16, name="ident_b")
         make_identity(nc, ident_b[:])
         make_identity(nc, ident_f[:])
+        w_nat = const.tile([P, 2, 2, FEAT], BF16, name="w_nat")
         wT = const.tile([P, 2, 2, FEAT], BF16, name="wT")
-        hc = const.tile([P, NPASS, FEAT], U32, name="hc", align_bytes=64)
-        hs = const.tile([P, NPASS, FEAT], U8, name="hs", align_bytes=64)
-        xT = const.tile([P, 2, ROWS], BF16, name="xT")
-        deg = const.tile([P, NBLK, 8], F32, name="deg")
-        sq = const.tile([P, NBLK], F32, name="sq")
-        dinv = const.tile([P, NBLK], F32, name="dinv")
+        hc = const.tile([P, CHUNKS, FEAT], U32, name="hc", align_bytes=64)
+        hs = const.tile([P, CHUNKS, FEAT], U8, name="hs", align_bytes=64)
+        xT = const.tile([P, 2, NODES], BF16, name="xT")
+        drow = const.tile([P, NODES], F32, name="drow")
+        deg = const.tile([P, 4 * CHUNKS, 8], F32, name="deg")
+        sq = const.tile([P, 4 * CHUNKS], F32, name="sq")
+        dinv = const.tile([P, 4 * CHUNKS], F32, name="dinv")
         warm = const.tile([P, 1], F32, name="warm")
         nc.vector.memset(warm[:], 1.0)
         nc.scalar.activation(out=warm[:], in_=warm[:], func=ACT.Sqrt)
 
-        first = {}
-        second = {}
-        st = {"x": None}
+        tiles = {}
+        loaded = []
 
-        scratch = apool.tile([P, 2, NODES], BF16, name="scratch", tag="a", align_bytes=64)
-        w_nat = scratch[:, 0, 3072:4096].rearrange("p (w h d) -> p w h d", w=2, h=2)
-        xT_tail = scratch[:, 0, 0:2048].rearrange("p (h n) -> p h n", h=2)
         nc.sync.dma_start(out=w_nat[:, 0], in_=W_gcn.rearrange("(h p) d -> p h d", p=P))
         nc.sync.dma_start(out=w_nat[:, 1], in_=W_skip.rearrange("(h p) d -> p h d", p=P))
+        x_half = []
+        for q in range(2):
+            x_t = spool.tile([P, 4, T, FEAT], BF16, name="x_t", tag="s", align_bytes=64)
+            nc.sync.dma_start(out=x_t[:], in_=x_rows[:, 4 * q : 4 * q + 4])
+            x_half.append(x_t)
 
-        def load_x():
-            x_t = apool.tile([P, 2, NODES], BF16, name="x_t", tag="a", align_bytes=64)
-            st["x"] = x_t[:].rearrange("p a n -> p (a n)")
-            nc.sync.dma_start(out=st["x"].rearrange("p (g t d) -> p g t d", t=4, d=FEAT), in_=x_groups)
+        def load(b):
+            g, t = b // T, b % T
+            if b < RES_TILES:
+                a_t = rpool.tile([P, NODES], BF16, name="a_r", tag="r", align_bytes=64)
+            else:
+                a_t = spool.tile([P, NODES], BF16, name="a_s", tag="s", align_bytes=64)
+            nc.sync.dma_start(out=a_t[:], in_=a_rows[g][:, t, :])
+            tiles[b] = a_t
 
-        def load_chunk(c, again):
-            for G in range(2 * c, 2 * c + 2):
-                a_t = apool.tile([P, 2, NODES], BF16, name="a_t", tag="a", align_bytes=64)
-                nc.sync.dma_start(out=a_t[:], in_=a_groups[c, G % 2])
-                for e in range(2):
-                    (second if again else first)[2 * G + e] = a_t[:, e, :]
+        for b in range(RES_TILES):
+            load(b)
 
-        def degrees(c):
-            for blk in range(4 * c, 4 * c + 4):
-                a_b = first[blk]
-                if blk % 2 == 0:
-                    nc.vector.tensor_scalar(out=a_b, in0=a_b, scalar1=1.0, scalar2=None, op0=ALU.mult, op1=ALU.add, accum_out=deg[:, blk, 0:1])
-                else:
-                    nc.scalar.activation(out=a_b, in_=a_b, func=ACT.Copy, accum_out=deg[:, blk, 0:1])
-            cols = slice(4 * c, 4 * c + 4)
-            nc.scalar.activation(out=sq[:, cols], in_=deg[:, cols, 0], func=ACT.Sqrt, bias=1e-8)
-            nc.vector.reciprocal(out=dinv[:, cols], in_=sq[:, cols])
-
-        def features():
-            x_flat = st["x"]
-            wps = psum.tile([P, 2, 2, 2, P], BF16, name="wps", tag="T")
+        def weights():
+            wps = psum_t.tile([P, 2, 2, 2, P], BF16, name="wps", tag="T")
             for w in range(2):
                 for dh in range(2):
                     for oh in range(2):
                         nc.tensor.transpose(wps[:, w, dh, oh, :], w_nat[:, w, oh, P * dh : P * dh + P], ident_b[:])
             nc.scalar.copy(out=wT[:].rearrange("p w h o -> p (w h o)"), in_=wps[:].rearrange("p w h q o -> p (w h q o)"))
-            for q in range(4):
-                for dh in range(2):
-                    xps = psum.tile([P, 8, P], BF16, name="xps", tag="T")
-                    for nb in range(8):
-                        col = FEAT * (8 * q + nb) + P * dh
-                        nc.tensor.transpose(xps[:, nb, :], x_flat[:, col : col + P], ident_b[:])
-                    dst = xT[:, dh, 1024 * q : 1024 * q + 1024] if q < 3 else xT_tail[:, dh, :]
-                    if dh == 0:
-                        nc.scalar.copy(out=dst, in_=xps[:].rearrange("p b n -> p (b n)"))
-                    else:
-                        nc.vector.tensor_copy(out=dst, in_=xps[:].rearrange("p b n -> p (b n)"))
-            for g in range(NPASS):
-                gh = x_flat[:, 1024 * g : 1024 * g + 1024].rearrange("p (c t) -> p c t", t=4)
-                for ch in range(2):
-                    hps = psum.tile([P, 4, P], F32, name="hps", tag="T")
-                    for t in range(4):
-                        blk = 4 * g + t
-                        for dh in range(2):
-                            lhsT = xT[:, dh, P * blk : P * blk + P] if blk < MBLK else xT_tail[:, dh, P * (blk - MBLK) : P * (blk - MBLK) + P]
-                            nc.tensor.matmul(out=hps[:, t, :], lhsT=lhsT, rhs=wT[:, 0, dh, P * ch : P * ch + P], start=(dh == 0), stop=(dh == 1))
-                    nc.vector.tensor_copy(out=gh[:, P * ch : P * ch + P, :], in_=hps[:].rearrange("p t c -> p c t"))
-                nc.vector.quantize_mx(out=hc[:, g, :].bitcast(FP8X4), scales=hs[:, g, :], in_=x_flat[:, 1024 * g : 1024 * g + 1024])
 
-        toks = make_tokens()
-        pairs = [t for t in toks if t[0] == "pair"]
-        work = [{} for t in pairs]
-        acc = {}
-        seen = {}
-        drow = {}
-        wsm = {}
-        fin = []
+        def x_turn(g):
+            for dh in range(2):
+                xps = psum_t.tile([P, T, P], BF16, name="xps", tag="T")
+                for t in range(T):
+                    nc.tensor.transpose(xps[:, t, :], x_half[g // 4][:, g % 4, t, P * dh : P * dh + P], ident_b[:])
+                nc.scalar.copy(out=xT[:, dh, 512 * g : 512 * g + 512], in_=xps[:].rearrange("p t n -> p (t n)"))
 
-        def prep(m):
-            dps = psum.tile([P, 4, P], F32, name="dps", tag="T")
-            for j in range(4):
-                b = 4 * m + j
-                nc.tensor.transpose(dps[:, j, :], dinv[:, b : b + 1].to_broadcast([P, P]), ident_f[:])
-            dr = dpool.tile([P, PASS], F32, name="dr")
-            nc.scalar.copy(out=dr[:], in_=dps[:].rearrange("p j r -> p (j r)"))
-            drow[m] = dr
-            ws = []
+        def h_rows(g):
+            xg = x_half[g // 4][:, g % 4].rearrange("p t d -> p (t d)")
+            gh = xg.rearrange("p (c t) -> p c t", t=T)
             for ch in range(2):
-                skp = psum.tile([P, PASS], F32, name="skp", tag="T")
-                for dh in range(2):
-                    nc.tensor.matmul(out=skp[:], lhsT=wT[:, 1, dh, P * ch : P * ch + P], rhs=xT[:, dh, PASS * m : PASS * m + PASS], start=(dh == 0), stop=(dh == 1))
-                w = epool.tile([P, PASS], F32, name="w%d" % ch)
-                nc.scalar.activation(out=w[:], in_=skp[:], func=ACT.Copy, scale=0.5)
-                ws.append(w)
-            wsm[m] = ws
+                hps = psum_t.tile([P, T, P], F32, name="hps", tag="T")
+                for t in range(T):
+                    col = 512 * g + P * t
+                    for dh in range(2):
+                        nc.tensor.matmul(out=hps[:, t, :], lhsT=xT[:, dh, col : col + P], rhs=wT[:, 0, dh, P * ch : P * ch + P], start=(dh == 0), stop=(dh == 1))
+                src = hps[:].rearrange("p t c -> p c t")
+                nc.vector.tensor_copy(out=gh[:, P * ch : P * ch + P, :], in_=src)
+            nc.vector.quantize_mx(out=hc[:, g, :].bitcast(FP8X4), scales=hs[:, g, :], in_=xg)
 
-        def stage_t(k):
-            if k >= len(pairs):
-                return
-            m, g, ph = pairs[k][1], pairs[k][2], pairs[k][3]
-            src = second if ph == 2 else first
-            banks = []
-            for u in range(2):
-                bank = psum.tile([P, 4, P], F32, name="bank", tag="T")
-                for j in range(4):
-                    nc.tensor.transpose(bank[:, j, :], src[4 * m + j].bitcast(F32)[:, 256 * g + u : 256 * g + 256 : 2], ident_f[:])
-                banks.append(bank)
-            work[k]["banks"] = banks
-
-        def stage_v(k):
-            m, g = pairs[k][1], pairs[k][2]
-            planes = ppool.tile([P, 4, PASS], BF16, name="planes")
-            for u in range(2):
-                halves = work[k]["banks"][u][:].rearrange("p j r -> p (j r)").bitcast(BF16).rearrange("p (x e) -> p x e", e=2)
-                for e in range(2):
-                    t = 2 * u + e
-                    nc.vector.scalar_tensor_tensor(out=planes[:, t, :], in0=halves[:, :, e], scalar=dinv[:, 4 * g + t : 4 * g + t + 1], in1=drow[m][:], op0=ALU.mult, op1=ALU.mult)
-            work[k]["planes"] = planes
-
-        def stage_r(k):
-            planes = work[k]["planes"]
-            grp = gpool.tile([P, PASS, 4], BF16, name="grp", align_bytes=64)
-            if pairs[k][3] == 1:
-                nc.gpsimd.tensor_scalar(out=grp[:], in0=planes[:].rearrange("p t x -> p x t"), scalar1=1.0, scalar2=0.0, op0=ALU.mult, op1=ALU.add)
+        def row_sum(b):
+            a_b = tiles[b][:]
+            if b % 2 == 0:
+                nc.vector.tensor_scalar(out=a_b, in0=a_b, scalar1=1.0, scalar2=None, op0=ALU.mult, op1=ALU.add, accum_out=deg[:, b, 0:1])
             else:
-                nc.scalar.copy(out=grp[:].rearrange("p (c i) t -> p c t i", i=4), in_=planes[:].rearrange("p t (c i) -> p c t i", i=4))
-            work[k]["grp"] = grp
+                nc.scalar.activation(out=a_b, in_=a_b, func=ACT.Copy, accum_out=deg[:, b, 0:1])
 
-        def stage_q(k):
-            m, g = pairs[k][1], pairs[k][2]
-            if m not in acc:
-                acc[m] = [psum.tile([P, PASS], F32, name="acc", tag="acc") for ch in range(2)]
-            codes = cpool.tile([P, PASS], U32, name="codes", align_bytes=64)
-            scl = cpool.tile([P, PASS], U8, name="scl", align_bytes=64)
-            nc.vector.quantize_mx(out=codes[:].bitcast(FP8X4), scales=scl[:], in_=work[k]["grp"][:].rearrange("p x t -> p (x t)"))
-            seen[m] = seen.get(m, 0) + 1
-            for ch in range(2):
-                nc.tensor.matmul_mx(out=acc[m][ch][:], lhsT=hc[:, g, P * ch : P * ch + P].bitcast(FP8X4), lhsT_scale=hs[:, g, P * ch : P * ch + P], rhs=codes[:].bitcast(FP8X4), rhs_scale=scl[:], start=(seen[m] == 1), stop=(seen[m] == NPASS))
-            if seen[m] == NPASS:
-                fin.append((m, k + FIN_DELAY))
+        def d_root(g):
+            cols = slice(4 * g, 4 * g + 4)
+            nc.scalar.activation(out=sq[:, cols], in_=deg[:, cols, 0], func=ACT.Sqrt, bias=1e-8)
 
-        def finish(m):
-            ws = wsm[m]
-            for ch in range(2):
-                w = ws[ch]
-                nc.vector.scalar_tensor_tensor(out=w[:], in0=acc[m][ch][:], scalar=0.5, in1=w[:], op0=ALU.mult, op1=ALU.add)
-                nc.vector.scalar_tensor_tensor(out=w[:], in0=w[:], scalar=0.0, in1=xT[:, ch, PASS * m : PASS * m + PASS], op0=ALU.max, op1=ALU.add)
-            for jp in range(2):
-                bo = psum.tile([P, 2, 2, P], F32, name="bo", tag="T")
-                for e in range(2):
-                    for ch in range(2):
-                        col = P * (2 * jp + e)
-                        nc.tensor.transpose(bo[:, e, ch, :], ws[ch][:, col : col + P], ident_f[:])
-                o = epool.tile([P, 2, FEAT], F32, name="o")
-                nc.scalar.copy(out=o[:].rearrange("p e c -> p (e c)"), in_=bo[:].rearrange("p e h c -> p (e h c)"))
-                nc.scalar.dma_start(out=out_groups[m, jp], in_=o[:])
+        dps_of = {}
 
-        k = 0
-        qd = 0
-        for tok in toks:
-            kind = tok[0]
-            if kind == "loadx":
-                load_x()
-            elif kind == "load":
-                load_chunk(tok[1], tok[2])
-            elif kind == "feat":
-                features()
-            elif kind == "rows":
-                degrees(tok[1])
-            elif kind == "prep":
-                prep(tok[1])
-            elif kind == "pair":
-                if k == 0:
-                    stage_t(0)
-                stage_t(k + 1)
-                stage_v(k)
-                stage_r(k)
-                if k - LAG >= qd:
-                    stage_q(qd)
-                    qd += 1
-                k += 1
-                while fin and fin[0][1] <= k:
-                    finish(fin.pop(0)[0])
-            else:
-                while qd < k:
-                    stage_q(qd)
-                    qd += 1
-                while fin:
-                    finish(fin.pop(0)[0])
+        def d_inverse(g):
+            cols = slice(4 * g, 4 * g + 4)
+            nc.vector.reciprocal(out=dinv[:, cols], in_=sq[:, cols])
+            dps = psum_k.tile([P, T, P], F32, name="dps", tag="K")
+            for t in range(T):
+                b = 4 * g + t
+                nc.tensor.transpose(dps[:, t, :], dinv[:, b : b + 1].to_broadcast([P, P]), ident_f[:])
+            dps_of[g] = dps
+
+        def d_spread(g):
+            nc.scalar.copy(out=drow[:, 512 * g : 512 * g + 512].rearrange("p (n t) -> p n t", t=T), in_=dps_of[g][:].rearrange("p t n -> p n t"))
+
+        def scale(b, c0, c1):
+            a_b = tiles[b][:, c0:c1]
+            nc.vector.scalar_tensor_tensor(out=a_b, in0=a_b, scalar=dinv[:, b : b + 1], in1=drow[:, c0:c1], op0=ALU.mult, op1=ALU.mult)
+
+        banks = {}
+
+        def turn(b, q):
+            bank = psum_t.tile([P, 2, 2, P], F32, name="bank", tag="T")
+            words = tiles[b][:].bitcast(F32)
+            for s in range(2):
+                for u in range(2):
+                    w0 = 512 * q + 256 * s
+                    nc.tensor.transpose(bank[:, s, u, :], words[:, w0 + u : w0 + 256 : 2], ident_f[:])
+            banks[(b, q)] = bank
+
+        def regroup(b, q):
+            words = tiles[b][:].bitcast(F32)[:, 512 * q : 512 * q + 512]
+            nc.scalar.copy(out=words.rearrange("p (s r u) -> p s r u", s=2, u=2), in_=banks[(b, q)][:].rearrange("p s u r -> p s r u"))
+
+        pend_t = []
+        pend_c = []
+
+        def flush(n_t, n_c):
+            while len(pend_t) > n_t:
+                u = pend_t.pop(0)
+                turn(u[0], u[1])
+                pend_c.append(u)
+            while len(pend_c) > n_c:
+                u = pend_c.pop(0)
+                regroup(u[0], u[1])
+
+        done = {}
+
+        def unit(b, q):
+            scale(b, PAIR * q, PAIR * q + PAIR)
+            done[b] = q + 1
+            pend_t.append((b, q))
+            flush(LAG_T, LAG_C - LAG_T)
+
+        codes_of = {}
+        skip_of = {}
+        acc_of = {}
+        o_of = {}
+        xr_of = {}
+
+        def quantise(b):
+            codes = cpool.tile([P, CHUNKS * P], U32, name="codes", align_bytes=64)
+            scl = cpool.tile([P, CHUNKS * P], U8, name="scl", align_bytes=64)
+            nc.vector.quantize_mx(out=codes[:].bitcast(FP8X4), scales=scl[:], in_=tiles[b][:])
+            codes_of[b] = (codes, scl)
+
+        def skip(b):
+            if b % T == 0:
+                xr = epool.tile([P, T, FEAT], BF16, name="xr")
+                nc.sync.dma_start(out=xr[:], in_=x_rows[:, b // T])
+                xr_of[b // T] = xr
+            skp = psum_k.tile([P, FEAT], F32, name="skp", tag="K")
+            for dh in range(2):
+                nc.tensor.matmul(out=skp[:], lhsT=xT[:, dh, P * b : P * b + P], rhs=wT[:, 1, dh, :], start=(dh == 0), stop=(dh == 1))
+            w = epool.tile([P, FEAT], F32, name="w")
+            nc.scalar.activation(out=w[:], in_=skp[:], func=ACT.Copy, scale=0.5)
+            skip_of[b] = w
+
+        def product(b):
+            codes, scl = codes_of[b]
+            acc = psum_a.tile([P, FEAT], F32, name="acc", tag="acc")
+            for g in range(CHUNKS):
+                rows = slice(P * g, P * g + P)
+                nc.tensor.matmul_mx(out=acc[:], lhsT=codes[:, rows].bitcast(FP8X4), lhsT_scale=scl[:, rows], rhs=hc[:, g, :].bitcast(FP8X4), rhs_scale=hs[:, g, :], start=(g == 0), stop=(g == CHUNKS - 1))
+            acc_of[b] = acc
+
+        def add_skip(b):
+            w = skip_of[b]
+            nc.vector.scalar_tensor_tensor(out=w[:], in0=acc_of[b][:], scalar=0.5, in1=w[:], op0=ALU.mult, op1=ALU.add)
+
+        def finish(b):
+            w = skip_of[b]
+            nc.scalar.activation(out=w[:], in_=w[:], func=ACT.Relu)
+            if b % 2 == 0:
+                o_of[b // 2] = epool.tile([P, 2, FEAT], F32, name="o")
+            o = o_of[b // 2]
+            nc.gpsimd.tensor_tensor(out=o[:, b % 2], in0=w[:], in1=xr_of[b // T][:, b % T], op=ALU.add)
+            if b % 2 == 1:
+                t0 = b % T - 1
+                nc.sync.dma_start(out=out_rows[b // T][:, t0 : t0 + 2], in_=o[:])
+
+        weights()
+        for g in range(CHUNKS):
+            x_turn(g)
+        for g in range(CHUNKS):
+            h_rows(g)
+        work = []
+        for c in range(CHUNKS):
+            for t in range(T):
+                b = T * c + t
+                if b == RES_TILES:
+                    for k in range(b, b + 4):
+                        load(k)
+                row_sum(b)
+                if b >= RES_TILES and b + 4 < T * CHUNKS:
+                    load(b + 4)
+                if c > 0 and t == 0:
+                    d_inverse(c - 1)
+                if c > 0 and t == 1:
+                    d_spread(c - 1)
+                    if c == 2:
+                        work.extend([(r, 0) for r in range(8)])
+                    elif c == 4:
+                        work.extend([(r, 1) for r in range(8)])
+                        work.extend([(r, q) for r in range(8, 16) for q in range(2)])
+                    elif c == 6:
+                        work.extend([(r, 2) for r in range(16)])
+                for k in range(2):
+                    if work and t > 0:
+                        r, q = work.pop(0)
+                        unit(r, q)
+            d_root(c)
+        d_inverse(CHUNKS - 1)
+        d_spread(CHUNKS - 1)
+        flush(0, 0)
+
+        for b in range(RES_TILES, RES_TILES + 4):
+            load(b)
+
+        def s_scale(b):
+            q0 = done.get(b, 0)
+            scale(b, PAIR * q0, NODES)
+
+        def s_turn(b):
+            for q in range(done.get(b, 0), NPAIR):
+                pend_t.append((b, q))
+                flush(0, 0)
+
+        for n in range(OUT_TILES + 4):
+            if n < OUT_TILES:
+                s_scale(n)
+            if 0 <= n - 1 < OUT_TILES:
+                s_turn(n - 1)
+                skip(n - 1)
+            if 0 <= n - 2 < OUT_TILES:
+                quantise(n - 2)
+                if n - 2 >= RES_TILES and n + 2 < OUT_TILES:
+                    load(n + 2)
+                product(n - 2)
+            if 0 <= n - 3 < OUT_TILES:
+                add_skip(n - 3)
+                finish(n - 3)

@@ -21,8 +21,17 @@ OUT_TILES = ROWS // P
 RES_TILES = 16
 PAIR = 1024
 NPAIR = NODES // PAIR
-LAG_T = 1
-LAG_C = 2
+SUMS = ("VVSV", "VSVV", "SGVS", "GSGS") + ("SGSG",) * 4
+QUARTER = NODES // 4
+FOLD_LAG = 2
+PER_SLOT = 5
+PER_SUM = 2
+LAST = 8
+AHEAD = 3
+PLAG = 2
+XS = 1
+HS = 2
+STREAM = 4
 
 FLOPS = 2 * ROWS * NODES * FEAT + 2 * NODES * FEAT * FEAT + 2 * ROWS * FEAT * FEAT
 
@@ -35,13 +44,12 @@ def tile_structureawaregcn_t_kernel(tc, adjacency_matrix, node_features, W_gcn, 
     with ExitStack() as ctx:
         const = ctx.enter_context(tc.tile_pool(name="const", bufs=1))
         rpool = ctx.enter_context(tc.tile_pool(name="rpool", bufs=RES_TILES))
-        spool = ctx.enter_context(tc.tile_pool(name="spool", bufs=4))
-        cpool = ctx.enter_context(tc.tile_pool(name="cpool", bufs=2))
+        spool = ctx.enter_context(tc.tile_pool(name="spool", bufs=STREAM))
+        cpool = ctx.enter_context(tc.tile_pool(name="cpool", bufs=3))
+        gpool = ctx.enter_context(tc.tile_pool(name="gpool", bufs=2))
         epool = ctx.enter_context(tc.tile_pool(name="epool", bufs=3))
         psum_t = ctx.enter_context(tc.psum_pool(name="psum_t", bufs=4))
-        psum_a = ctx.enter_context(tc.psum_pool(name="psum_a", bufs=2))
-        psum_k = ctx.enter_context(tc.psum_pool(name="psum_k", bufs=2))
-        ctx.enter_context(tc.manual_schedule())
+        psum_x = ctx.enter_context(tc.psum_pool(name="psum_x", bufs=4))
 
         ident_f = const.tile([P, P], F32, name="ident_f")
         ident_b = const.tile([P, P], BF16, name="ident_b")
@@ -54,7 +62,8 @@ def tile_structureawaregcn_t_kernel(tc, adjacency_matrix, node_features, W_gcn, 
         xT = const.tile([P, 2, NODES], BF16, name="xT")
         drow = const.tile([P, NODES], F32, name="drow")
         deg = const.tile([P, 4 * CHUNKS, 8], F32, name="deg")
-        sq = const.tile([P, 4 * CHUNKS], F32, name="sq")
+        ones = const.tile([P, 2], F32, name="ones")
+        nc.vector.memset(ones[:], 1.0)
         dinv = const.tile([P, 4 * CHUNKS], F32, name="dinv")
         warm = const.tile([P, 1], F32, name="warm")
         nc.vector.memset(warm[:], 1.0)
@@ -66,10 +75,12 @@ def tile_structureawaregcn_t_kernel(tc, adjacency_matrix, node_features, W_gcn, 
         nc.sync.dma_start(out=w_nat[:, 0], in_=W_gcn.rearrange("(h p) d -> p h d", p=P))
         nc.sync.dma_start(out=w_nat[:, 1], in_=W_skip.rearrange("(h p) d -> p h d", p=P))
         x_half = []
-        for q in range(2):
-            x_t = spool.tile([P, 4, T, FEAT], BF16, name="x_t", tag="s", align_bytes=64)
-            nc.sync.dma_start(out=x_t[:], in_=x_rows[:, 4 * q : 4 * q + 4])
-            x_half.append(x_t)
+
+        def load_x():
+            for q in range(2):
+                x_t = spool.tile([P, 4, T, FEAT], BF16, name="x_t", tag="s", align_bytes=64)
+                nc.sync.dma_start(out=x_t[:], in_=x_rows[:, 4 * q : 4 * q + 4])
+                x_half.append(x_t)
 
         def load(b):
             g, t = b // T, b % T
@@ -80,7 +91,7 @@ def tile_structureawaregcn_t_kernel(tc, adjacency_matrix, node_features, W_gcn, 
             nc.sync.dma_start(out=a_t[:], in_=a_rows[g][:, t, :])
             tiles[b] = a_t
 
-        for b in range(RES_TILES):
+        for b in range(RES_TILES + STREAM):
             load(b)
 
         def weights():
@@ -96,7 +107,7 @@ def tile_structureawaregcn_t_kernel(tc, adjacency_matrix, node_features, W_gcn, 
                 xps = psum_t.tile([P, T, P], BF16, name="xps", tag="T")
                 for t in range(T):
                     nc.tensor.transpose(xps[:, t, :], x_half[g // 4][:, g % 4, t, P * dh : P * dh + P], ident_b[:])
-                nc.scalar.copy(out=xT[:, dh, 512 * g : 512 * g + 512], in_=xps[:].rearrange("p t n -> p (t n)"))
+                (nc.scalar.copy if XS else nc.vector.tensor_copy)(out=xT[:, dh, 512 * g : 512 * g + 512], in_=xps[:].rearrange("p t n -> p (t n)"))
 
         def h_rows(g):
             xg = x_half[g // 4][:, g % 4].rearrange("p t d -> p (t d)")
@@ -108,26 +119,56 @@ def tile_structureawaregcn_t_kernel(tc, adjacency_matrix, node_features, W_gcn, 
                     for dh in range(2):
                         nc.tensor.matmul(out=hps[:, t, :], lhsT=xT[:, dh, col : col + P], rhs=wT[:, 0, dh, P * ch : P * ch + P], start=(dh == 0), stop=(dh == 1))
                 src = hps[:].rearrange("p t c -> p c t")
-                nc.vector.tensor_copy(out=gh[:, P * ch : P * ch + P, :], in_=src)
-            nc.vector.quantize_mx(out=hc[:, g, :].bitcast(FP8X4), scales=hs[:, g, :], in_=xg)
+                (nc.scalar.copy if ch < HS else nc.vector.tensor_copy)(out=gh[:, P * ch : P * ch + P, :], in_=src)
+
+        def h_quantise(q):
+            gs = slice(4 * q, 4 * q + 4)
+            nc.vector.quantize_mx(out=hc[:, gs, :].rearrange("p g c -> p (g c)").bitcast(FP8X4), scales=hs[:, gs, :].rearrange("p g c -> p (g c)"), in_=x_half[q][:].rearrange("p g t d -> p (g t d)"))
+
+        part_of = {}
+
+        turned_of = {}
+
+        def fold_half(b, k):
+            part = part_of[b][k]
+            if k == 0:
+                turned_of[b] = psum_t.tile([P, P], F32, name="turned", tag="T")
+            blocks = QUARTER // P
+            for j in range(blocks):
+                nc.tensor.matmul(out=turned_of[b][:], lhsT=part[:, P * j : P * j + P], rhs=ident_f[:], start=(k == 0 and j == 0), stop=(k == 1 and j == blocks - 1), is_transpose=True)
 
         def row_sum(b):
             a_b = tiles[b][:]
-            if b % 2 == 0:
+            who = SUMS[b // T][b % T]
+            if who == "V":
                 nc.vector.tensor_scalar(out=a_b, in0=a_b, scalar1=1.0, scalar2=None, op0=ALU.mult, op1=ALU.add, accum_out=deg[:, b, 0:1])
-            else:
+            elif who == "S":
                 nc.scalar.activation(out=a_b, in_=a_b, func=ACT.Copy, accum_out=deg[:, b, 0:1])
+            else:
+                part_of[b] = []
+                for k in range(2):
+                    c0 = 2 * QUARTER * k
+                    part = gpool.tile([P, QUARTER], F32, name="part")
+                    nc.gpsimd.tensor_tensor(out=part[:], in0=a_b[:, c0 : c0 + QUARTER], in1=a_b[:, c0 + QUARTER : c0 + 2 * QUARTER], op=ALU.add)
+                    part_of[b].append(part)
+                    fold_half(b, k)
 
-        def d_root(g):
-            cols = slice(4 * g, 4 * g + 4)
-            nc.scalar.activation(out=sq[:, cols], in_=deg[:, cols, 0], func=ACT.Sqrt, bias=1e-8)
+        def fold(b):
+            if b in part_of:
+                turned = turned_of[b]
+                fsb = gpool.tile([P, P], F32, name="fsb")
+                nc.scalar.copy(out=fsb[:], in_=turned[:])
+                col = psum_t.tile([P, 2], F32, name="col", tag="T")
+                nc.tensor.matmul(out=col[:], lhsT=fsb[:], rhs=ones[:], start=True, stop=True)
+                nc.scalar.copy(out=deg[:, b, 0:1], in_=col[:, 0:1])
 
         dps_of = {}
 
-        def d_inverse(g):
+        def d_turn(g):
             cols = slice(4 * g, 4 * g + 4)
-            nc.vector.reciprocal(out=dinv[:, cols], in_=sq[:, cols])
-            dps = psum_k.tile([P, T, P], F32, name="dps", tag="K")
+            nc.scalar.activation(out=dinv[:, cols], in_=deg[:, cols, 0], func=ACT.Sqrt, bias=1e-8)
+            nc.vector.reciprocal(out=dinv[:, cols], in_=dinv[:, cols])
+            dps = psum_x.tile([P, T, P], F32, name="dps", tag="X")
             for t in range(T):
                 b = 4 * g + t
                 nc.tensor.transpose(dps[:, t, :], dinv[:, b : b + 1].to_broadcast([P, P]), ident_f[:])
@@ -155,30 +196,17 @@ def tile_structureawaregcn_t_kernel(tc, adjacency_matrix, node_features, W_gcn, 
             words = tiles[b][:].bitcast(F32)[:, 512 * q : 512 * q + 512]
             nc.scalar.copy(out=words.rearrange("p (s r u) -> p s r u", s=2, u=2), in_=banks[(b, q)][:].rearrange("p s u r -> p s r u"))
 
-        pend_t = []
-        pend_c = []
-
-        def flush(n_t, n_c):
-            while len(pend_t) > n_t:
-                u = pend_t.pop(0)
-                turn(u[0], u[1])
-                pend_c.append(u)
-            while len(pend_c) > n_c:
-                u = pend_c.pop(0)
-                regroup(u[0], u[1])
-
         done = {}
 
-        def unit(b, q):
-            scale(b, PAIR * q, PAIR * q + PAIR)
-            done[b] = q + 1
-            pend_t.append((b, q))
-            flush(LAG_T, LAG_C - LAG_T)
+        def unit(b, g0):
+            for g in (g0,):
+                a_b = tiles[b][:, 512 * g : 512 * g + 512].rearrange("p (n t) -> p n t", t=T)
+                nc.vector.scalar_tensor_tensor(out=a_b, in0=a_b, scalar=dinv[:, b : b + 1], in1=dps_of[g][:].rearrange("p t n -> p n t"), op0=ALU.mult, op1=ALU.mult)
+            done[b] = g0 + 1
 
         codes_of = {}
         skip_of = {}
         acc_of = {}
-        o_of = {}
         xr_of = {}
 
         def quantise(b):
@@ -188,11 +216,10 @@ def tile_structureawaregcn_t_kernel(tc, adjacency_matrix, node_features, W_gcn, 
             codes_of[b] = (codes, scl)
 
         def skip(b):
-            if b % T == 0:
-                xr = epool.tile([P, T, FEAT], BF16, name="xr")
-                nc.sync.dma_start(out=xr[:], in_=x_rows[:, b // T])
-                xr_of[b // T] = xr
-            skp = psum_k.tile([P, FEAT], F32, name="skp", tag="K")
+            xr = epool.tile([P, FEAT], BF16, name="xr")
+            nc.sync.dma_start(out=xr[:], in_=x_rows[:, b // T, b % T])
+            xr_of[b] = xr
+            skp = psum_x.tile([P, FEAT], F32, name="skp", tag="X")
             for dh in range(2):
                 nc.tensor.matmul(out=skp[:], lhsT=xT[:, dh, P * b : P * b + P], rhs=wT[:, 1, dh, :], start=(dh == 0), stop=(dh == 1))
             w = epool.tile([P, FEAT], F32, name="w")
@@ -201,7 +228,7 @@ def tile_structureawaregcn_t_kernel(tc, adjacency_matrix, node_features, W_gcn, 
 
         def product(b):
             codes, scl = codes_of[b]
-            acc = psum_a.tile([P, FEAT], F32, name="acc", tag="acc")
+            acc = psum_x.tile([P, FEAT], F32, name="acc", tag="X")
             for g in range(CHUNKS):
                 rows = slice(P * g, P * g + P)
                 nc.tensor.matmul_mx(out=acc[:], lhsT=codes[:, rows].bitcast(FP8X4), lhsT_scale=scl[:, rows], rhs=hc[:, g, :].bitcast(FP8X4), rhs_scale=hs[:, g, :], start=(g == 0), stop=(g == CHUNKS - 1))
@@ -214,72 +241,79 @@ def tile_structureawaregcn_t_kernel(tc, adjacency_matrix, node_features, W_gcn, 
         def finish(b):
             w = skip_of[b]
             nc.scalar.activation(out=w[:], in_=w[:], func=ACT.Relu)
-            if b % 2 == 0:
-                o_of[b // 2] = epool.tile([P, 2, FEAT], F32, name="o")
-            o = o_of[b // 2]
-            nc.gpsimd.tensor_tensor(out=o[:, b % 2], in0=w[:], in1=xr_of[b // T][:, b % T], op=ALU.add)
-            if b % 2 == 1:
-                t0 = b % T - 1
-                nc.sync.dma_start(out=out_rows[b // T][:, t0 : t0 + 2], in_=o[:])
+            o = epool.tile([P, FEAT], F32, name="o")
+            nc.gpsimd.tensor_tensor(out=o[:], in0=w[:], in1=xr_of[b][:], op=ALU.add)
+            nc.sync.dma_start(out=out_rows[b // T][:, b % T], in_=o[:])
 
-        weights()
-        for g in range(CHUNKS):
-            x_turn(g)
-        for g in range(CHUNKS):
-            h_rows(g)
         work = []
-        for c in range(CHUNKS):
-            for t in range(T):
-                b = T * c + t
-                if b == RES_TILES:
-                    for k in range(b, b + 4):
-                        load(k)
-                row_sum(b)
-                if b >= RES_TILES and b + 4 < T * CHUNKS:
-                    load(b + 4)
-                if c > 0 and t == 0:
-                    d_inverse(c - 1)
-                if c > 0 and t == 1:
-                    d_spread(c - 1)
-                    if c == 2:
-                        work.extend([(r, 0) for r in range(8)])
-                    elif c == 4:
-                        work.extend([(r, 1) for r in range(8)])
-                        work.extend([(r, q) for r in range(8, 16) for q in range(2)])
-                    elif c == 6:
-                        work.extend([(r, 2) for r in range(16)])
-                for k in range(2):
-                    if work and t > 0:
-                        r, q = work.pop(0)
-                        unit(r, q)
-            d_root(c)
-        d_inverse(CHUNKS - 1)
-        d_spread(CHUNKS - 1)
-        flush(0, 0)
+        stages = T * CHUNKS + FOLD_LAG + 2
+        for s in range(stages):
+            if s < T * CHUNKS:
+                row_sum(s)
+                if s >= RES_TILES and s + STREAM < T * CHUNKS:
+                    load(s + STREAM)
+            f = s - FOLD_LAG
+            if 0 <= f < T * CHUNKS:
+                fold(f)
+            c = f // T
+            if f > 0 and f % T == T - 1 and c < CHUNKS:
+                d_turn(c)
+                d_spread(c)
+                work.extend([(r, g) for g in range(c) for r in range(T * c, min(T * c + T, RES_TILES))])
+                work.extend([(r, c) for r in range(min(T * c + T, RES_TILES))])
+            for k in range(PER_SUM if s < T * CHUNKS and SUMS[s // T][s % T] == "V" else PER_SLOT):
+                if work and c < LAST:
+                    r, q = work.pop(0)
+                    unit(r, q)
+        for r, q in work:
+            if q < LAST:
+                unit(r, q)
 
-        for b in range(RES_TILES, RES_TILES + 4):
+        load_x()
+        weights()
+        for g in range(CHUNKS + 1):
+            if g < CHUNKS:
+                x_turn(g)
+            if g > 0:
+                h_rows(g - 1)
+            if g == 4:
+                h_quantise(0)
+        h_quantise(1)
+
+        for b in range(RES_TILES, RES_TILES + STREAM):
             load(b)
 
-        def s_scale(b):
-            q0 = done.get(b, 0)
-            scale(b, PAIR * q0, NODES)
+        order = []
+        for k in range(OUT_TILES - RES_TILES):
+            order.extend([2 * k, 2 * k + 1, RES_TILES + k])
+        pieces = []
+        for b in order:
+            for q in range(done.get(b, 0) // 2, NPAIR):
+                pieces.append((b, max(done.get(b, 0) * 512, PAIR * q), PAIR * q + PAIR))
+        scaled = 0
 
-        def s_turn(b):
-            for q in range(done.get(b, 0), NPAIR):
-                pend_t.append((b, q))
-                flush(0, 0)
-
-        for n in range(OUT_TILES + 4):
-            if n < OUT_TILES:
-                s_scale(n)
+        ctx.enter_context(tc.manual_schedule())
+        for n in range(-AHEAD, OUT_TILES + PLAG + 1):
             if 0 <= n - 1 < OUT_TILES:
-                s_turn(n - 1)
-                skip(n - 1)
-            if 0 <= n - 2 < OUT_TILES:
-                quantise(n - 2)
-                if n - 2 >= RES_TILES and n + 2 < OUT_TILES:
-                    load(n + 2)
-                product(n - 2)
-            if 0 <= n - 3 < OUT_TILES:
-                add_skip(n - 3)
-                finish(n - 3)
+                quantise(order[n - 1])
+            m = n - PLAG - 1
+            if 0 <= m < OUT_TILES:
+                add_skip(order[m])
+            goal = -(-len(pieces) * (n + AHEAD + 1) // (OUT_TILES + AHEAD))
+            needed = order[: max(0, min(n + 2, OUT_TILES))]
+            while scaled < len(pieces) and (scaled < goal or pieces[scaled][0] in needed):
+                b, c0, c1 = pieces[scaled]
+                scale(b, c0, c1)
+                scaled += 1
+            if 0 <= n < OUT_TILES:
+                for q in range(NPAIR):
+                    turn(order[n], q)
+                    regroup(order[n], q)
+            if 0 <= n - PLAG < OUT_TILES:
+                b = order[n - PLAG]
+                if b >= RES_TILES and b + STREAM < OUT_TILES:
+                    load(b + STREAM)
+                skip(b)
+                product(b)
+            if 0 <= m < OUT_TILES:
+                finish(order[m])

@@ -21,7 +21,7 @@ OUT_TILES = ROWS // P
 RES_TILES = 16
 PAIR = 1024
 NPAIR = NODES // PAIR
-SUMS = ("VVSV", "VSVV", "SGVS", "GSGS") + ("SGSG",) * 4
+SUMS = ("VVSV", "VSVV", "SVGV", "SVGV") + ("GSGS",) * 4
 QUARTER = NODES // 4
 FOLD_LAG = 2
 PER_SLOT = 5

@@ -21,13 +21,20 @@ OUT_TILES = ROWS // P
 RES_TILES = 16
 PAIR = 1024
 NPAIR = NODES // PAIR
-SUMS = ("VVSV", "VSVV", "SVGV", "SVGV") + ("GSGS",) * 4
+SUMS = ("VVSV", "VSVV", "SPGV", "SPGV") + ("GSGS",) * 4
 QUARTER = NODES // 4
 FOLD_LAG = 2
 PER_SLOT = 5
 PER_SUM = 2
-LAST = 8
-AHEAD = 3
+LAST = 6
+READY_LAG = 2
+EARLY_FROM = 99
+EARLY = 1
+X_LOAD = 4
+X_SLOT = 4
+EARLY_HALVES = 0
+PIECE = 2048
+AHEAD = 10
 PLAG = 2
 XS = 1
 HS = 2
@@ -76,11 +83,10 @@ def tile_structureawaregcn_t_kernel(tc, adjacency_matrix, node_features, W_gcn, 
         nc.sync.dma_start(out=w_nat[:, 1], in_=W_skip.rearrange("(h p) d -> p h d", p=P))
         x_half = []
 
-        def load_x():
-            for q in range(2):
-                x_t = spool.tile([P, 4, T, FEAT], BF16, name="x_t", tag="s", align_bytes=64)
-                nc.sync.dma_start(out=x_t[:], in_=x_rows[:, 4 * q : 4 * q + 4])
-                x_half.append(x_t)
+        def load_x(q):
+            x_t = spool.tile([P, 4, T, FEAT], BF16, name="x_t", tag="s", align_bytes=64)
+            nc.sync.dma_start(out=x_t[:], in_=x_rows[:, 4 * q : 4 * q + 4])
+            x_half.append(x_t)
 
         def load(b):
             g, t = b // T, b % T
@@ -92,6 +98,9 @@ def tile_structureawaregcn_t_kernel(tc, adjacency_matrix, node_features, W_gcn, 
             tiles[b] = a_t
 
         for b in range(RES_TILES + STREAM):
+            if b == X_LOAD:
+                for q in range(EARLY_HALVES):
+                    load_x(q)
             load(b)
 
         def weights():
@@ -137,11 +146,26 @@ def tile_structureawaregcn_t_kernel(tc, adjacency_matrix, node_features, W_gcn, 
             for j in range(blocks):
                 nc.tensor.matmul(out=turned_of[b][:], lhsT=part[:, P * j : P * j + P], rhs=ident_f[:], start=(k == 0 and j == 0), stop=(k == 1 and j == blocks - 1), is_transpose=True)
 
+        def features(q):
+            if q == 0:
+                weights()
+            for g in range(4 * q, 4 * q + 5):
+                if g < 4 * q + 4:
+                    x_turn(g)
+                if g > 4 * q:
+                    h_rows(g - 1)
+            h_quantise(q)
+
         def row_sum(b):
             a_b = tiles[b][:]
             who = SUMS[b // T][b % T]
             if who == "V":
                 nc.vector.tensor_scalar(out=a_b, in0=a_b, scalar1=1.0, scalar2=None, op0=ALU.mult, op1=ALU.add, accum_out=deg[:, b, 0:1])
+            elif who == "P":
+                folded = psum_t.tile([P, 512], F32, name="folded", tag="T")
+                for j in range(CHUNKS):
+                    nc.tensor.matmul(out=folded[:], lhsT=ident_b[:], rhs=a_b[:, 512 * j : 512 * j + 512], start=(j == 0), stop=(j == CHUNKS - 1))
+                nc.scalar.activation(out=drow[:, 3584:4096], in_=folded[:], func=ACT.Copy, accum_out=deg[:, b, 0:1])
             elif who == "S":
                 nc.scalar.activation(out=a_b, in_=a_b, func=ACT.Copy, accum_out=deg[:, b, 0:1])
             else:
@@ -197,12 +221,25 @@ def tile_structureawaregcn_t_kernel(tc, adjacency_matrix, node_features, W_gcn, 
             nc.scalar.copy(out=words.rearrange("p (s r u) -> p s r u", s=2, u=2), in_=banks[(b, q)][:].rearrange("p s u r -> p s r u"))
 
         done = {}
+        ready = []
+        turned_pairs = {}
+
+        def early(count):
+            for k in range(count):
+                if len(ready) > READY_LAG:
+                    b, q = ready.pop(0)
+                    turn(b, q)
+                    regroup(b, q)
+                    turned_pairs[b] = q + 1
+
 
         def unit(b, g0):
             for g in (g0,):
                 a_b = tiles[b][:, 512 * g : 512 * g + 512].rearrange("p (n t) -> p n t", t=T)
                 nc.vector.scalar_tensor_tensor(out=a_b, in0=a_b, scalar=dinv[:, b : b + 1], in1=dps_of[g][:].rearrange("p t n -> p n t"), op0=ALU.mult, op1=ALU.mult)
             done[b] = g0 + 1
+            if g0 % 2 == 1:
+                ready.append((b, g0 // 2))
 
         codes_of = {}
         skip_of = {}
@@ -248,6 +285,9 @@ def tile_structureawaregcn_t_kernel(tc, adjacency_matrix, node_features, W_gcn, 
         work = []
         stages = T * CHUNKS + FOLD_LAG + 2
         for s in range(stages):
+            if s == X_SLOT:
+                for q in range(EARLY_HALVES):
+                    features(q)
             if s < T * CHUNKS:
                 row_sum(s)
                 if s >= RES_TILES and s + STREAM < T * CHUNKS:
@@ -265,20 +305,15 @@ def tile_structureawaregcn_t_kernel(tc, adjacency_matrix, node_features, W_gcn, 
                 if work and c < LAST:
                     r, q = work.pop(0)
                     unit(r, q)
+            if s >= EARLY_FROM:
+                early(EARLY)
         for r, q in work:
             if q < LAST:
                 unit(r, q)
 
-        load_x()
-        weights()
-        for g in range(CHUNKS + 1):
-            if g < CHUNKS:
-                x_turn(g)
-            if g > 0:
-                h_rows(g - 1)
-            if g == 4:
-                h_quantise(0)
-        h_quantise(1)
+        for q in range(EARLY_HALVES, 2):
+            load_x(q)
+            features(q)
 
         for b in range(RES_TILES, RES_TILES + STREAM):
             load(b)
@@ -288,8 +323,11 @@ def tile_structureawaregcn_t_kernel(tc, adjacency_matrix, node_features, W_gcn, 
             order.extend([2 * k, 2 * k + 1, RES_TILES + k])
         pieces = []
         for b in order:
-            for q in range(done.get(b, 0) // 2, NPAIR):
-                pieces.append((b, max(done.get(b, 0) * 512, PAIR * q), PAIR * q + PAIR))
+            c0 = 512 * done.get(b, 0)
+            while c0 < NODES:
+                c1 = min(NODES, c0 - c0 % PIECE + PIECE)
+                pieces.append((b, c0, c1))
+                c0 = c1
         scaled = 0
 
         ctx.enter_context(tc.manual_schedule())
@@ -306,7 +344,7 @@ def tile_structureawaregcn_t_kernel(tc, adjacency_matrix, node_features, W_gcn, 
                 scale(b, c0, c1)
                 scaled += 1
             if 0 <= n < OUT_TILES:
-                for q in range(NPAIR):
+                for q in range(turned_pairs.get(order[n], 0), NPAIR):
                     turn(order[n], q)
                     regroup(order[n], q)
             if 0 <= n - PLAG < OUT_TILES:

@@ -27,18 +27,13 @@ FOLD_LAG = 2
 PER_SLOT = 5
 PER_SUM = 2
 LAST = 6
-READY_LAG = 2
-EARLY_FROM = 99
-EARLY = 1
-X_LOAD = 4
-X_SLOT = 4
-EARLY_HALVES = 0
 PIECE = 2048
-AHEAD = 10
+AHEAD = 8
 PLAG = 2
-XS = 1
-HS = 2
 STREAM = 4
+PATTERN = 0
+TAIL_V = 1
+TAIL_Q = 0
 
 FLOPS = 2 * ROWS * NODES * FEAT + 2 * NODES * FEAT * FEAT + 2 * ROWS * FEAT * FEAT
 
@@ -55,6 +50,7 @@ def tile_structureawaregcn_t_kernel(tc, adjacency_matrix, node_features, W_gcn, 
         cpool = ctx.enter_context(tc.tile_pool(name="cpool", bufs=3))
         gpool = ctx.enter_context(tc.tile_pool(name="gpool", bufs=2))
         epool = ctx.enter_context(tc.tile_pool(name="epool", bufs=3))
+        xrpool = ctx.enter_context(tc.tile_pool(name="xrpool", bufs=5))
         psum_t = ctx.enter_context(tc.psum_pool(name="psum_t", bufs=4))
         psum_x = ctx.enter_context(tc.psum_pool(name="psum_x", bufs=4))
 
@@ -68,7 +64,7 @@ def tile_structureawaregcn_t_kernel(tc, adjacency_matrix, node_features, W_gcn, 
         hs = const.tile([P, CHUNKS, FEAT], U8, name="hs", align_bytes=64)
         xT = const.tile([P, 2, NODES], BF16, name="xT")
         drow = const.tile([P, NODES], F32, name="drow")
-        deg = const.tile([P, 4 * CHUNKS, 8], F32, name="deg")
+        deg = const.tile([P, 4 * CHUNKS, 2], F32, name="deg")
         ones = const.tile([P, 2], F32, name="ones")
         nc.vector.memset(ones[:], 1.0)
         dinv = const.tile([P, 4 * CHUNKS], F32, name="dinv")
@@ -77,7 +73,6 @@ def tile_structureawaregcn_t_kernel(tc, adjacency_matrix, node_features, W_gcn, 
         nc.scalar.activation(out=warm[:], in_=warm[:], func=ACT.Sqrt)
 
         tiles = {}
-        loaded = []
 
         nc.sync.dma_start(out=w_nat[:, 0], in_=W_gcn.rearrange("(h p) d -> p h d", p=P))
         nc.sync.dma_start(out=w_nat[:, 1], in_=W_skip.rearrange("(h p) d -> p h d", p=P))
@@ -98,9 +93,6 @@ def tile_structureawaregcn_t_kernel(tc, adjacency_matrix, node_features, W_gcn, 
             tiles[b] = a_t
 
         for b in range(RES_TILES + STREAM):
-            if b == X_LOAD:
-                for q in range(EARLY_HALVES):
-                    load_x(q)
             load(b)
 
         def weights():
@@ -116,7 +108,7 @@ def tile_structureawaregcn_t_kernel(tc, adjacency_matrix, node_features, W_gcn, 
                 xps = psum_t.tile([P, T, P], BF16, name="xps", tag="T")
                 for t in range(T):
                     nc.tensor.transpose(xps[:, t, :], x_half[g // 4][:, g % 4, t, P * dh : P * dh + P], ident_b[:])
-                (nc.scalar.copy if XS else nc.vector.tensor_copy)(out=xT[:, dh, 512 * g : 512 * g + 512], in_=xps[:].rearrange("p t n -> p (t n)"))
+                nc.scalar.copy(out=xT[:, dh, 512 * g : 512 * g + 512], in_=xps[:].rearrange("p t n -> p (t n)"))
 
         def h_rows(g):
             xg = x_half[g // 4][:, g % 4].rearrange("p t d -> p (t d)")
@@ -128,7 +120,7 @@ def tile_structureawaregcn_t_kernel(tc, adjacency_matrix, node_features, W_gcn, 
                     for dh in range(2):
                         nc.tensor.matmul(out=hps[:, t, :], lhsT=xT[:, dh, col : col + P], rhs=wT[:, 0, dh, P * ch : P * ch + P], start=(dh == 0), stop=(dh == 1))
                 src = hps[:].rearrange("p t c -> p c t")
-                (nc.scalar.copy if ch < HS else nc.vector.tensor_copy)(out=gh[:, P * ch : P * ch + P, :], in_=src)
+                nc.scalar.copy(out=gh[:, P * ch : P * ch + P, :], in_=src)
 
         def h_quantise(q):
             gs = slice(4 * q, 4 * q + 4)
@@ -180,7 +172,7 @@ def tile_structureawaregcn_t_kernel(tc, adjacency_matrix, node_features, W_gcn, 
         def fold(b):
             if b in part_of:
                 turned = turned_of[b]
-                fsb = gpool.tile([P, P], F32, name="fsb")
+                fsb = cpool.tile([P, P], F32, name="fsb", tag="l", align_bytes=64)
                 nc.scalar.copy(out=fsb[:], in_=turned[:])
                 col = psum_t.tile([P, 2], F32, name="col", tag="T")
                 nc.tensor.matmul(out=col[:], lhsT=fsb[:], rhs=ones[:], start=True, stop=True)
@@ -221,41 +213,32 @@ def tile_structureawaregcn_t_kernel(tc, adjacency_matrix, node_features, W_gcn, 
             nc.scalar.copy(out=words.rearrange("p (s r u) -> p s r u", s=2, u=2), in_=banks[(b, q)][:].rearrange("p s u r -> p s r u"))
 
         done = {}
-        ready = []
-        turned_pairs = {}
 
-        def early(count):
-            for k in range(count):
-                if len(ready) > READY_LAG:
-                    b, q = ready.pop(0)
-                    turn(b, q)
-                    regroup(b, q)
-                    turned_pairs[b] = q + 1
-
-
-        def unit(b, g0):
-            for g in (g0,):
-                a_b = tiles[b][:, 512 * g : 512 * g + 512].rearrange("p (n t) -> p n t", t=T)
-                nc.vector.scalar_tensor_tensor(out=a_b, in0=a_b, scalar=dinv[:, b : b + 1], in1=dps_of[g][:].rearrange("p t n -> p n t"), op0=ALU.mult, op1=ALU.mult)
-            done[b] = g0 + 1
-            if g0 % 2 == 1:
-                ready.append((b, g0 // 2))
+        def unit(b, g):
+            a_b = tiles[b][:, 512 * g : 512 * g + 512].rearrange("p (n t) -> p n t", t=T)
+            nc.vector.scalar_tensor_tensor(out=a_b, in0=a_b, scalar=dinv[:, b : b + 1], in1=dps_of[g][:].rearrange("p t n -> p n t"), op0=ALU.mult, op1=ALU.mult)
+            done[b] = g + 1
 
         codes_of = {}
         skip_of = {}
         acc_of = {}
         xr_of = {}
 
-        def quantise(b):
-            codes = cpool.tile([P, CHUNKS * P], U32, name="codes", align_bytes=64)
-            scl = cpool.tile([P, CHUNKS * P], U8, name="scl", align_bytes=64)
-            nc.vector.quantize_mx(out=codes[:].bitcast(FP8X4), scales=scl[:], in_=tiles[b][:])
-            codes_of[b] = (codes, scl)
+        def quantise(b, q0=0, q1=NPAIR):
+            if q0 == 0:
+                codes = cpool.tile([P, CHUNKS * P], U32, name="codes", align_bytes=64)
+                scl = cpool.tile([P, CHUNKS * P], U8, name="scl", tag="l", align_bytes=64)
+                codes_of[b] = (codes, scl)
+            codes, scl = codes_of[b]
+            w = slice(2 * P * q0, 2 * P * q1)
+            nc.vector.quantize_mx(out=codes[:, w].bitcast(FP8X4), scales=scl[:, w], in_=tiles[b][:, PAIR * q0 : PAIR * q1])
 
-        def skip(b):
-            xr = epool.tile([P, FEAT], BF16, name="xr")
+        def load_rows(b):
+            xr = xrpool.tile([P, FEAT], BF16, name="xr")
             nc.sync.dma_start(out=xr[:], in_=x_rows[:, b // T, b % T])
             xr_of[b] = xr
+
+        def skip(b):
             skp = psum_x.tile([P, FEAT], F32, name="skp", tag="X")
             for dh in range(2):
                 nc.tensor.matmul(out=skp[:], lhsT=xT[:, dh, P * b : P * b + P], rhs=wT[:, 1, dh, :], start=(dh == 0), stop=(dh == 1))
@@ -277,17 +260,17 @@ def tile_structureawaregcn_t_kernel(tc, adjacency_matrix, node_features, W_gcn, 
 
         def finish(b):
             w = skip_of[b]
-            nc.scalar.activation(out=w[:], in_=w[:], func=ACT.Relu)
             o = epool.tile([P, FEAT], F32, name="o")
-            nc.gpsimd.tensor_tensor(out=o[:], in0=w[:], in1=xr_of[b][:], op=ALU.add)
+            if b == order[-1] and TAIL_V:
+                nc.vector.scalar_tensor_tensor(out=o[:], in0=w[:], scalar=0.0, in1=xr_of[b][:], op0=ALU.max, op1=ALU.add)
+            else:
+                nc.scalar.activation(out=w[:], in_=w[:], func=ACT.Relu)
+                nc.gpsimd.tensor_tensor(out=o[:], in0=w[:], in1=xr_of[b][:], op=ALU.add)
             nc.sync.dma_start(out=out_rows[b // T][:, b % T], in_=o[:])
 
         work = []
         stages = T * CHUNKS + FOLD_LAG + 2
         for s in range(stages):
-            if s == X_SLOT:
-                for q in range(EARLY_HALVES):
-                    features(q)
             if s < T * CHUNKS:
                 row_sum(s)
                 if s >= RES_TILES and s + STREAM < T * CHUNKS:
@@ -305,13 +288,11 @@ def tile_structureawaregcn_t_kernel(tc, adjacency_matrix, node_features, W_gcn, 
                 if work and c < LAST:
                     r, q = work.pop(0)
                     unit(r, q)
-            if s >= EARLY_FROM:
-                early(EARLY)
         for r, q in work:
             if q < LAST:
                 unit(r, q)
 
-        for q in range(EARLY_HALVES, 2):
+        for q in range(2):
             load_x(q)
             features(q)
 
@@ -320,7 +301,7 @@ def tile_structureawaregcn_t_kernel(tc, adjacency_matrix, node_features, W_gcn, 
 
         order = []
         for k in range(OUT_TILES - RES_TILES):
-            order.extend([2 * k, 2 * k + 1, RES_TILES + k])
+            order.extend([[2 * k, 2 * k + 1, RES_TILES + k], [2 * k, RES_TILES + k, 2 * k + 1], [RES_TILES + k, 2 * k, 2 * k + 1]][PATTERN])
         pieces = []
         for b in order:
             c0 = 512 * done.get(b, 0)
@@ -332,7 +313,7 @@ def tile_structureawaregcn_t_kernel(tc, adjacency_matrix, node_features, W_gcn, 
 
         ctx.enter_context(tc.manual_schedule())
         for n in range(-AHEAD, OUT_TILES + PLAG + 1):
-            if 0 <= n - 1 < OUT_TILES:
+            if 0 <= n - 1 < OUT_TILES and not (TAIL_Q and n == OUT_TILES):
                 quantise(order[n - 1])
             m = n - PLAG - 1
             if 0 <= m < OUT_TILES:
@@ -344,9 +325,12 @@ def tile_structureawaregcn_t_kernel(tc, adjacency_matrix, node_features, W_gcn, 
                 scale(b, c0, c1)
                 scaled += 1
             if 0 <= n < OUT_TILES:
-                for q in range(turned_pairs.get(order[n], 0), NPAIR):
+                load_rows(order[n])
+                for q in range(NPAIR):
                     turn(order[n], q)
                     regroup(order[n], q)
+                    if TAIL_Q and n == OUT_TILES - 1:
+                        quantise(order[n], q, q + 1)
             if 0 <= n - PLAG < OUT_TILES:
                 b = order[n - PLAG]
                 if b >= RES_TILES and b + STREAM < OUT_TILES:

@@ -28,7 +28,7 @@ PER_SLOT = 5
 PER_SUM = 2
 LAST = 6
 PIECE = 2048
-AHEAD = 8
+AHEAD = 10
 PLAG = 2
 STREAM = 4
 PATTERN = 0

@@ -21,7 +21,7 @@ OUT_TILES = ROWS // P
 RES_TILES = 16
 PAIR = 1024
 NPAIR = NODES // PAIR
-SUMS = ("VVSV", "VSVV", "SPGV", "SPGV") + ("GSGS",) * 4
+SUMS = ("VVSV", "VSVV", "QPGV", "SPGV", "GSGS", "GSGS", "GSGS", "GSGV")
 QUARTER = NODES // 4
 FOLD_LAG = 2
 PER_SLOT = 5
@@ -153,11 +153,16 @@ def tile_structureawaregcn_t_kernel(tc, adjacency_matrix, node_features, W_gcn, 
             who = SUMS[b // T][b % T]
             if who == "V":
                 nc.vector.tensor_scalar(out=a_b, in0=a_b, scalar1=1.0, scalar2=None, op0=ALU.mult, op1=ALU.add, accum_out=deg[:, b, 0:1])
-            elif who == "P":
+            elif who in "PQ":
                 folded = psum_t.tile([P, 512], F32, name="folded", tag="T")
-                for j in range(CHUNKS):
-                    nc.tensor.matmul(out=folded[:], lhsT=ident_b[:], rhs=a_b[:, 512 * j : 512 * j + 512], start=(j == 0), stop=(j == CHUNKS - 1))
+                last = CHUNKS - 1 if who == "P" else CHUNKS - 2
+                for j in range(last + 1):
+                    nc.tensor.matmul(out=folded[:], lhsT=ident_b[:], rhs=a_b[:, 512 * j : 512 * j + 512], start=(j == 0), stop=(j == last))
                 nc.scalar.activation(out=drow[:, 3584:4096], in_=folded[:], func=ACT.Copy, accum_out=deg[:, b, 0:1])
+                if who == "Q":
+                    rest = a_b[:, 3584:4096]
+                    nc.scalar.activation(out=rest, in_=rest, func=ACT.Copy, accum_out=deg[:, b, 1:2])
+                    nc.scalar.activation(out=deg[:, b, 0:1], in_=deg[:, b, 0:1], func=ACT.Identity, bias=deg[:, b, 1:2])
             elif who == "S":
                 nc.scalar.activation(out=a_b, in_=a_b, func=ACT.Copy, accum_out=deg[:, b, 0:1])
             else:
@@ -273,8 +278,8 @@ def tile_structureawaregcn_t_kernel(tc, adjacency_matrix, node_features, W_gcn, 
         for s in range(stages):
             if s < T * CHUNKS:
                 row_sum(s)
-                if s >= RES_TILES and s + STREAM < T * CHUNKS:
-                    load(s + STREAM)
+            if RES_TILES <= s < T * CHUNKS - STREAM:
+                load(s + STREAM)
             f = s - FOLD_LAG
             if 0 <= f < T * CHUNKS:
                 fold(f)

@@ -30,7 +30,7 @@ LAST = 6
 PIECE = 2048
 AHEAD = 10
 PLAG = 2
-STREAM = 4
+STREAM = 5
 PATTERN = 0
 TAIL_V = 1
 TAIL_Q = 0
@@ -48,7 +48,6 @@ def tile_structureawaregcn_t_kernel(tc, adjacency_matrix, node_features, W_gcn, 
         rpool = ctx.enter_context(tc.tile_pool(name="rpool", bufs=RES_TILES))
         spool = ctx.enter_context(tc.tile_pool(name="spool", bufs=STREAM))
         cpool = ctx.enter_context(tc.tile_pool(name="cpool", bufs=3))
-        gpool = ctx.enter_context(tc.tile_pool(name="gpool", bufs=2))
         epool = ctx.enter_context(tc.tile_pool(name="epool", bufs=3))
         xrpool = ctx.enter_context(tc.tile_pool(name="xrpool", bufs=5))
         psum_t = ctx.enter_context(tc.psum_pool(name="psum_t", bufs=4))
@@ -169,7 +168,7 @@ def tile_structureawaregcn_t_kernel(tc, adjacency_matrix, node_features, W_gcn, 
                 part_of[b] = []
                 for k in range(2):
                     c0 = 2 * QUARTER * k
-                    part = gpool.tile([P, QUARTER], F32, name="part")
+                    part = cpool.tile([P, QUARTER], F32, name="part", tag="c", align_bytes=64)
                     nc.gpsimd.tensor_tensor(out=part[:], in0=a_b[:, c0 : c0 + QUARTER], in1=a_b[:, c0 + QUARTER : c0 + 2 * QUARTER], op=ALU.add)
                     part_of[b].append(part)
                     fold_half(b, k)
@@ -231,7 +230,7 @@ def tile_structureawaregcn_t_kernel(tc, adjacency_matrix, node_features, W_gcn, 
 
         def quantise(b, q0=0, q1=NPAIR):
             if q0 == 0:
-                codes = cpool.tile([P, CHUNKS * P], U32, name="codes", align_bytes=64)
+                codes = cpool.tile([P, CHUNKS * P], U32, name="codes", tag="c", align_bytes=64)
                 scl = cpool.tile([P, CHUNKS * P], U8, name="scl", tag="l", align_bytes=64)
                 codes_of[b] = (codes, scl)
             codes, scl = codes_of[b]

from contextlib import ExitStack

import concourse.mybir as mybir
from concourse.masks import make_identity

F32 = mybir.dt.float32
BF16 = mybir.dt.bfloat16
U8 = mybir.dt.uint8
U32 = mybir.dt.uint32
FP8X4 = mybir.dt.float8_e4m3fn_x4
ALU = mybir.AluOpType
ACT = mybir.ActivationFunctionType

P = 128
NODES = 4096
FEAT = 256
ROWS = 3072
T = 4
CHUNKS = NODES // (P * T)
OUT_TILES = ROWS // P
RES_TILES = 16
PAIR = 1024
NPAIR = NODES // PAIR
SUMS = ("VVSV", "VSVV", "QPGV", "SPGV", "GSGS", "GSGS", "GSGS", "GSGV")
QUARTER = NODES // 4
FOLD_LAG = 2
PER_SLOT = 5
PER_SUM = 2
LAST = 6
PIECE = 2048
AHEAD = 10
PLAG = 2
STREAM = 5
PATTERN = 0
TAIL_V = 1
TAIL_Q = 0

FLOPS = 2 * ROWS * NODES * FEAT + 2 * NODES * FEAT * FEAT + 2 * ROWS * FEAT * FEAT


def tile_structureawaregcn_t_kernel(tc, adjacency_matrix, node_features, W_gcn, W_skip, batch_size, out):
    nc = tc.nc
    a_rows = adjacency_matrix.rearrange("(g p t) n -> g p t n", p=P, t=T)
    x_rows = node_features.rearrange("(g p t) d -> p g t d", p=P, t=T)
    out_rows = out.rearrange("(g p t) c -> g p t c", p=P, t=T)
    with ExitStack() as ctx:
        const = ctx.enter_context(tc.tile_pool(name="const", bufs=1))
        rpool = ctx.enter_context(tc.tile_pool(name="rpool", bufs=RES_TILES))
        spool = ctx.enter_context(tc.tile_pool(name="spool", bufs=STREAM))
        cpool = ctx.enter_context(tc.tile_pool(name="cpool", bufs=3))
        epool = ctx.enter_context(tc.tile_pool(name="epool", bufs=3))
        xrpool = ctx.enter_context(tc.tile_pool(name="xrpool", bufs=5))
        psum_t = ctx.enter_context(tc.psum_pool(name="psum_t", bufs=4))
        psum_x = ctx.enter_context(tc.psum_pool(name="psum_x", bufs=4))

        ident_f = const.tile([P, P], F32, name="ident_f")
        ident_b = const.tile([P, P], BF16, name="ident_b")
        make_identity(nc, ident_b[:])
        make_identity(nc, ident_f[:])
        w_nat = const.tile([P, 2, 2, FEAT], BF16, name="w_nat")
        wT = const.tile([P, 2, 2, FEAT], BF16, name="wT")
        hc = const.tile([P, CHUNKS, FEAT], U32, name="hc", align_bytes=64)
        hs = const.tile([P, CHUNKS, FEAT], U8, name="hs", align_bytes=64)
        xT = const.tile([P, 2, NODES], BF16, name="xT")
        drow = const.tile([P, NODES], F32, name="drow")
        deg = const.tile([P, 4 * CHUNKS, 2], F32, name="deg")
        ones = const.tile([P, 2], F32, name="ones")
        nc.vector.memset(ones[:], 1.0)
        dinv = const.tile([P, 4 * CHUNKS], F32, name="dinv")
        warm = const.tile([P, 1], F32, name="warm")
        nc.vector.memset(warm[:], 1.0)
        nc.scalar.activation(out=warm[:], in_=warm[:], func=ACT.Sqrt)

        tiles = {}

        nc.sync.dma_start(out=w_nat[:, 0], in_=W_gcn.rearrange("(h p) d -> p h d", p=P))
        nc.sync.dma_start(out=w_nat[:, 1], in_=W_skip.rearrange("(h p) d -> p h d", p=P))
        x_half = []

        def load_x(q):
            x_t = spool.tile([P, 4, T, FEAT], BF16, name="x_t", tag="s", align_bytes=64)
            nc.sync.dma_start(out=x_t[:], in_=x_rows[:, 4 * q : 4 * q + 4])
            x_half.append(x_t)

        def load(b):
            g, t = b // T, b % T
            if b < RES_TILES:
                a_t = rpool.tile([P, NODES], BF16, name="a_r", tag="r", align_bytes=64)
            else:
                a_t = spool.tile([P, NODES], BF16, name="a_s", tag="s", align_bytes=64)
            nc.sync.dma_start(out=a_t[:], in_=a_rows[g][:, t, :])
            tiles[b] = a_t

        for b in range(RES_TILES + STREAM):
            load(b)

        def weights():
            wps = psum_t.tile([P, 2, 2, 2, P], BF16, name="wps", tag="T")
            for w in range(2):
                for dh in range(2):
                    for oh in range(2):
                        nc.tensor.transpose(wps[:, w, dh, oh, :], w_nat[:, w, oh, P * dh : P * dh + P], ident_b[:])
            nc.scalar.copy(out=wT[:].rearrange("p w h o -> p (w h o)"), in_=wps[:].rearrange("p w h q o -> p (w h q o)"))

        def x_turn(g):
            for dh in range(2):
                xps = psum_t.tile([P, T, P], BF16, name="xps", tag="T")
                for t in range(T):
                    nc.tensor.transpose(xps[:, t, :], x_half[g // 4][:, g % 4, t, P * dh : P * dh + P], ident_b[:])
                nc.scalar.copy(out=xT[:, dh, 512 * g : 512 * g + 512], in_=xps[:].rearrange("p t n -> p (t n)"))

        def h_rows(g):
            xg = x_half[g // 4][:, g % 4].rearrange("p t d -> p (t d)")
            gh = xg.rearrange("p (c t) -> p c t", t=T)
            for ch in range(2):
                hps = psum_t.tile([P, T, P], F32, name="hps", tag="T")
                for t in range(T):
                    col = 512 * g + P * t
                    for dh in range(2):
                        nc.tensor.matmul(out=hps[:, t, :], lhsT=xT[:, dh, col : col + P], rhs=wT[:, 0, dh, P * ch : P * ch + P], start=(dh == 0), stop=(dh == 1))
                src = hps[:].rearrange("p t c -> p c t")
                nc.scalar.copy(out=gh[:, P * ch : P * ch + P, :], in_=src)

        def h_quantise(q):
            gs = slice(4 * q, 4 * q + 4)
            nc.vector.quantize_mx(out=hc[:, gs, :].rearrange("p g c -> p (g c)").bitcast(FP8X4), scales=hs[:, gs, :].rearrange("p g c -> p (g c)"), in_=x_half[q][:].rearrange("p g t d -> p (g t d)"))

        part_of = {}

        turned_of = {}

        def fold_half(b, k):
            part = part_of[b][k]
            if k == 0:
                turned_of[b] = psum_t.tile([P, P], F32, name="turned", tag="T")
            blocks = QUARTER // P
            for j in range(blocks):
                nc.tensor.matmul(out=turned_of[b][:], lhsT=part[:, P * j : P * j + P], rhs=ident_f[:], start=(k == 0 and j == 0), stop=(k == 1 and j == blocks - 1), is_transpose=True)

        def features(q):
            if q == 0:
                weights()
            for g in range(4 * q, 4 * q + 5):
                if g < 4 * q + 4:
                    x_turn(g)
                if g > 4 * q:
                    h_rows(g - 1)
            h_quantise(q)

        def row_sum(b):
            a_b = tiles[b][:]
            who = SUMS[b // T][b % T]
            if who == "V":
                nc.vector.tensor_scalar(out=a_b, in0=a_b, scalar1=1.0, scalar2=None, op0=ALU.mult, op1=ALU.add, accum_out=deg[:, b, 0:1])
            elif who in "PQ":
                folded = psum_t.tile([P, 512], F32, name="folded", tag="T")
                last = CHUNKS - 1 if who == "P" else CHUNKS - 2
                for j in range(last + 1):
                    nc.tensor.matmul(out=folded[:], lhsT=ident_b[:], rhs=a_b[:, 512 * j : 512 * j + 512], start=(j == 0), stop=(j == last))
                nc.scalar.activation(out=drow[:, 3584:4096], in_=folded[:], func=ACT.Copy, accum_out=deg[:, b, 0:1])
                if who == "Q":
                    rest = a_b[:, 3584:4096]
                    nc.scalar.activation(out=rest, in_=rest, func=ACT.Copy, accum_out=deg[:, b, 1:2])
                    nc.scalar.activation(out=deg[:, b, 0:1], in_=deg[:, b, 0:1], func=ACT.Identity, bias=deg[:, b, 1:2])
            elif who == "S":
                nc.scalar.activation(out=a_b, in_=a_b, func=ACT.Copy, accum_out=deg[:, b, 0:1])
            else:
                part_of[b] = []
                for k in range(2):
                    c0 = 2 * QUARTER * k
                    part = cpool.tile([P, QUARTER], F32, name="part", tag="c", align_bytes=64)
                    nc.gpsimd.tensor_tensor(out=part[:], in0=a_b[:, c0 : c0 + QUARTER], in1=a_b[:, c0 + QUARTER : c0 + 2 * QUARTER], op=ALU.add)
                    part_of[b].append(part)
                    fold_half(b, k)

        def fold(b):
            if b in part_of:
                turned = turned_of[b]
                fsb = cpool.tile([P, P], F32, name="fsb", tag="l", align_bytes=64)
                nc.scalar.copy(out=fsb[:], in_=turned[:])
                col = psum_t.tile([P, 2], F32, name="col", tag="T")
                nc.tensor.matmul(out=col[:], lhsT=fsb[:], rhs=ones[:], start=True, stop=True)
                nc.scalar.copy(out=deg[:, b, 0:1], in_=col[:, 0:1])

        dps_of = {}

        def d_turn(g):
            cols = slice(4 * g, 4 * g + 4)
            nc.scalar.activation(out=dinv[:, cols], in_=deg[:, cols, 0], func=ACT.Sqrt, bias=1e-8)
            nc.vector.reciprocal(out=dinv[:, cols], in_=dinv[:, cols])
            dps = psum_x.tile([P, T, P], F32, name="dps", tag="X")
            for t in range(T):
                b = 4 * g + t
                nc.tensor.transpose(dps[:, t, :], dinv[:, b : b + 1].to_broadcast([P, P]), ident_f[:])
            dps_of[g] = dps

        def d_spread(g):
            nc.scalar.copy(out=drow[:, 512 * g : 512 * g + 512].rearrange("p (n t) -> p n t", t=T), in_=dps_of[g][:].rearrange("p t n -> p n t"))

        def scale(b, c0, c1):
            a_b = tiles[b][:, c0:c1]
            nc.vector.scalar_tensor_tensor(out=a_b, in0=a_b, scalar=dinv[:, b : b + 1], in1=drow[:, c0:c1], op0=ALU.mult, op1=ALU.mult)

        banks = {}

        def turn(b, q):
            bank = psum_t.tile([P, 2, 2, P], F32, name="bank", tag="T")
            words = tiles[b][:].bitcast(F32)
            for s in range(2):
                for u in range(2):
                    w0 = 512 * q + 256 * s
                    nc.tensor.transpose(bank[:, s, u, :], words[:, w0 + u : w0 + 256 : 2], ident_f[:])
            banks[(b, q)] = bank

        def regroup(b, q):
            words = tiles[b][:].bitcast(F32)[:, 512 * q : 512 * q + 512]
            nc.scalar.copy(out=words.rearrange("p (s r u) -> p s r u", s=2, u=2), in_=banks[(b, q)][:].rearrange("p s u r -> p s r u"))

        done = {}

        def unit(b, g):
            a_b = tiles[b][:, 512 * g : 512 * g + 512].rearrange("p (n t) -> p n t", t=T)
            nc.vector.scalar_tensor_tensor(out=a_b, in0=a_b, scalar=dinv[:, b : b + 1], in1=dps_of[g][:].rearrange("p t n -> p n t"), op0=ALU.mult, op1=ALU.mult)
            done[b] = g + 1

        codes_of = {}
        skip_of = {}
        acc_of = {}
        xr_of = {}

        def quantise(b, q0=0, q1=NPAIR):
            if q0 == 0:
                codes = cpool.tile([P, CHUNKS * P], U32, name="codes", tag="c", align_bytes=64)
                scl = cpool.tile([P, CHUNKS * P], U8, name="scl", tag="l", align_bytes=64)
                codes_of[b] = (codes, scl)
            codes, scl = codes_of[b]
            w = slice(2 * P * q0, 2 * P * q1)
            nc.vector.quantize_mx(out=codes[:, w].bitcast(FP8X4), scales=scl[:, w], in_=tiles[b][:, PAIR * q0 : PAIR * q1])

        def load_rows(b):
            xr = xrpool.tile([P, FEAT], BF16, name="xr")
            nc.sync.dma_start(out=xr[:], in_=x_rows[:, b // T, b % T])
            xr_of[b] = xr

        def skip(b):
            skp = psum_x.tile([P, FEAT], F32, name="skp", tag="X")
            for dh in range(2):
                nc.tensor.matmul(out=skp[:], lhsT=xT[:, dh, P * b : P * b + P], rhs=wT[:, 1, dh, :], start=(dh == 0), stop=(dh == 1))
            w = epool.tile([P, FEAT], F32, name="w")
            nc.scalar.activation(out=w[:], in_=skp[:], func=ACT.Copy, scale=0.5)
            skip_of[b] = w

        def product(b):
            codes, scl = codes_of[b]
            acc = psum_x.tile([P, FEAT], F32, name="acc", tag="X")
            for g in range(CHUNKS):
                rows = slice(P * g, P * g + P)
                nc.tensor.matmul_mx(out=acc[:], lhsT=codes[:, rows].bitcast(FP8X4), lhsT_scale=scl[:, rows], rhs=hc[:, g, :].bitcast(FP8X4), rhs_scale=hs[:, g, :], start=(g == 0), stop=(g == CHUNKS - 1))
            acc_of[b] = acc

        def add_skip(b):
            w = skip_of[b]
            nc.vector.scalar_tensor_tensor(out=w[:], in0=acc_of[b][:], scalar=0.5, in1=w[:], op0=ALU.mult, op1=ALU.add)

        def finish(b):
            w = skip_of[b]
            o = epool.tile([P, FEAT], F32, name="o")
            if b == order[-1] and TAIL_V:
                nc.vector.scalar_tensor_tensor(out=o[:], in0=w[:], scalar=0.0, in1=xr_of[b][:], op0=ALU.max, op1=ALU.add)
            else:
                nc.scalar.activation(out=w[:], in_=w[:], func=ACT.Relu)
                nc.gpsimd.tensor_tensor(out=o[:], in0=w[:], in1=xr_of[b][:], op=ALU.add)
            nc.sync.dma_start(out=out_rows[b // T][:, b % T], in_=o[:])

        work = []
        stages = T * CHUNKS + FOLD_LAG + 2
        for s in range(stages):
            if s < T * CHUNKS:
                row_sum(s)
            if RES_TILES <= s < T * CHUNKS - STREAM:
                load(s + STREAM)
            f = s - FOLD_LAG
            if 0 <= f < T * CHUNKS:
                fold(f)
            c = f // T
            if f > 0 and f % T == T - 1 and c < CHUNKS:
                d_turn(c)
                d_spread(c)
                work.extend([(r, g) for g in range(c) for r in range(T * c, min(T * c + T, RES_TILES))])
                work.extend([(r, c) for r in range(min(T * c + T, RES_TILES))])
            for k in range(PER_SUM if s < T * CHUNKS and SUMS[s // T][s % T] == "V" else PER_SLOT):
                if work and c < LAST:
                    r, q = work.pop(0)
                    unit(r, q)
        for r, q in work:
            if q < LAST:
                unit(r, q)

        for q in range(2):
            load_x(q)
            features(q)

        for b in range(RES_TILES, RES_TILES + STREAM):
            load(b)

        order = []
        for k in range(OUT_TILES - RES_TILES):
            order.extend([[2 * k, 2 * k + 1, RES_TILES + k], [2 * k, RES_TILES + k, 2 * k + 1], [RES_TILES + k, 2 * k, 2 * k + 1]][PATTERN])
        pieces = []
        for b in order:
            c0 = 512 * done.get(b, 0)
            while c0 < NODES:
                c1 = min(NODES, c0 - c0 % PIECE + PIECE)
                pieces.append((b, c0, c1))
                c0 = c1
        scaled = 0

        ctx.enter_context(tc.manual_schedule())
        for n in range(-AHEAD, OUT_TILES + PLAG + 1):
            if 0 <= n - 1 < OUT_TILES and not (TAIL_Q and n == OUT_TILES):
                quantise(order[n - 1])
            m = n - PLAG - 1
            if 0 <= m < OUT_TILES:
                add_skip(order[m])
            goal = -(-len(pieces) * (n + AHEAD + 1) // (OUT_TILES + AHEAD))
            needed = order[: max(0, min(n + 2, OUT_TILES))]
            while scaled < len(pieces) and (scaled < goal or pieces[scaled][0] in needed):
                b, c0, c1 = pieces[scaled]
                scale(b, c0, c1)
                scaled += 1
            if 0 <= n < OUT_TILES:
                load_rows(order[n])
                for q in range(NPAIR):
                    turn(order[n], q)
                    regroup(order[n], q)
                    if TAIL_Q and n == OUT_TILES - 1:
                        quantise(order[n], q, q + 1)
            if 0 <= n - PLAG < OUT_TILES:
                b = order[n - PLAG]
                if b >= RES_TILES and b + STREAM < OUT_TILES:
                    load(b + STREAM)
                skip(b)
                product(b)
            if 0 <= m < OUT_TILES:
                finish(order[m])
